import numpy as np
import ml_dtypes


def mxq(x, axis, fmt="e4m3"):
    dtype, down = {"e4m3": (ml_dtypes.float8_e4m3fn, 7), "e5m2": (ml_dtypes.float8_e5m2, 14)}[fmt]
    v = np.moveaxis(np.asarray(x, np.float32).astype(ml_dtypes.bfloat16).astype(np.float64), axis, -1)
    blocks = v.reshape(v.shape[:-1] + (-1, 32))
    amax = np.abs(blocks).max(-1, keepdims=True)
    byte = np.maximum(np.where(amax > 0, np.frexp(amax)[1] - 1 + 127, 0) - down, 1)
    scale = np.exp2(byte - 127.0)
    codes = (blocks / scale).astype(np.float32).astype(dtype).astype(np.float64)
    return np.moveaxis((codes * scale).reshape(v.shape), -1, axis)


WIDE = False


def mx_kscale(k):
    if not WIDE:
        return np.ones(k)
    levels = np.array([10, -10, 5, -5, 0])
    a = np.random.permutation(np.resize(levels, k // 512 * 4)).reshape(k // 512, 4)
    idx = np.arange(k)
    return np.exp2(a[idx // 512, idx % 128 // 32])


BF16 = ml_dtypes.bfloat16


def bf(x):
    return np.asarray(x, np.float32).astype(BF16)


def f64(x):
    return np.asarray(x).astype(np.float64)


N, S, I, L, M = 128, 8, 512, 512, 256
D = I + L


def sigmoid(v):
    return 1.0 / (1.0 + np.exp(-v))


def setup_inputs():
    s = mx_kscale(D)
    r = np.random.standard_normal
    return {"modulation": bf((r((N, S, I)) * s[:I]).reshape(N, S * I)),
            "h0": bf((r((N, S, L)) * s[I:]).reshape(N, S * L)),
            "c0": bf(r((N, S * L))),
            "Wi": bf(r((S, L, D)) / np.sqrt(D) / s), "b_i": bf(-1.0 + 0.3 * r((S, L))),
            "Wf": bf(r((S, L, D)) / np.sqrt(D) / s), "b_f": bf(1.0 + 0.3 * r((S, L))),
            "Wg": bf(r((S, L, D)) / np.sqrt(D) / s), "b_g": bf(0.3 * r((S, L)))}


def proj(xq, W, b):
    return (xq.transpose(1, 0, 2) @ mxq(f64(W), 2, "e4m3").transpose(0, 2, 1)).transpose(1, 0, 2) + f64(b)


def reference(modulation, h0, c0, Wi, b_i, Wf, b_f, Wg, b_g):
    x = f64(modulation).reshape(N, S, I)
    h = f64(h0).reshape(N, S, L)
    c = f64(c0).reshape(N, S, L)
    xq = mxq(np.concatenate([x, h], axis=-1), 2, "e4m3")
    i = sigmoid(proj(xq, Wi, b_i))
    f = sigmoid(proj(xq, Wf, b_f))
    g = np.tanh(proj(xq, Wg, b_g))
    return (f * c + i * g).reshape(N, S * L)

@@ -1,0 +1,216 @@
+from contextlib import ExitStack
+
+import concourse.bass as bass
+import concourse.mybir as mybir
+import concourse.tile as tile
+from concourse.masks import make_identity
+
+F32 = mybir.dt.float32
+BF16 = mybir.dt.bfloat16
+U32 = mybir.dt.uint32
+U8 = mybir.dt.uint8
+FP8X4 = mybir.dt.float8_e4m3fn_x4
+ACT = mybir.ActivationFunctionType
+ALU = mybir.AluOpType
+
+P = 128
+STREAMS = 8
+GATES = 3
+UNITS = STREAMS * GATES
+FLOPS = 2 * 128 * STREAMS * GATES * 512 * 1024
+RAW_BUFS = 12
+
+
+def tile_flatlstm_pa_kernel(tc, modulation, h0, c0, Wi, b_i, Wf, b_f, Wg, b_g, out):
+    nc = tc.nc
+    weights = (Wi, Wf, Wg)
+    biases = (b_i, b_f, b_g)
+    funcs = (ACT.Sigmoid, ACT.Sigmoid, ACT.Tanh)
+    with ExitStack() as ctx:
+        const = ctx.enter_context(tc.tile_pool(name="const", bufs=1))
+        rawp = ctx.enter_context(tc.tile_pool(name="rawp", bufs=RAW_BUFS))
+        grpp = ctx.enter_context(tc.tile_pool(name="grpp", bufs=3))
+        codep = ctx.enter_context(tc.tile_pool(name="codep", bufs=3))
+        gatep = ctx.enter_context(tc.tile_pool(name="gatep", bufs=2))
+        ps_tp = ctx.enter_context(tc.psum_pool(name="ps_tp", bufs=4))
+        ps_acc = ctx.enter_context(tc.psum_pool(name="ps_acc", bufs=2))
+        ps_tb = ctx.enter_context(tc.psum_pool(name="ps_tb", bufs=2))
+        ctx.enter_context(tc.manual_schedule())
+
+        ident = const.tile([P, P], F32, name="ident")
+        x_sb = const.tile([P, 4096], BF16, name="x_sb")
+        h_sb = const.tile([P, 4096], BF16, name="h_sb")
+        c_sb = const.tile([P, 4096], BF16, name="c_sb")
+        o_sb = const.tile([P, 4096], F32, name="o_sb")
+        x_codes = const.tile([P, 2048], U32, name="x_codes", align_bytes=64)
+        x_scales = const.tile([P, 2048], U8, name="x_scales", align_bytes=64)
+        b_rows = const.tile([P, 512], BF16, name="b_rows")
+        b_f32 = const.tile([P, 512], F32, name="b_f32")
+        bias_sb = const.tile([P, 4 * 24], F32, name="bias_sb")
+        warm = const.tile([P, 2], F32, name="warm")
+
+        xf = x_sb[:].bitcast(F32)
+        hf = h_sb[:].bitcast(F32)
+
+        raw = {}
+
+        def load_w(u):
+            s, g = divmod(u, GATES)
+            t = rawp.tile([P, 4096], BF16, name="raw")
+            nc.sync.dma_start(out=t[:], in_=weights[g][s].rearrange("(p t) d -> p (t d)", t=4))
+            raw[u] = t
+
+        def load_xh(half):
+            cols = slice(half * 2048, (half + 1) * 2048)
+            nc.sync.dma_start(out=x_sb[:, cols], in_=modulation[:, cols])
+            nc.sync.dma_start(out=h_sb[:, cols], in_=h0[:, cols])
+
+        nc.vector.memset(warm[:], 0.0)
+        nc.vector.memset(b_rows[:], 0.0)
+        for g in range(GATES):
+            nc.scalar.dma_start(out=b_rows[8 * g:8 * g + 8, :], in_=biases[g])
+        nc.scalar.activation(out=warm[:, 1:2], in_=warm[:, 0:1], func=ACT.Sigmoid)
+        make_identity(nc, ident[:])
+
+        load_xh(0)
+        for u in range(3):
+            load_w(u)
+        nc.sync.dma_start(out=c_sb[:], in_=c0)
+        for u in range(3, 6):
+            load_w(u)
+        load_xh(1)
+        for u in range(6, RAW_BUFS):
+            load_w(u)
+
+        def transpose_bank(srcs):
+            tp = ps_tp.tile([P, 512], F32, name="tp")
+            for q in range(4):
+                nc.tensor.transpose(out=tp[:, q * P:(q + 1) * P], in_=srcs[q], identity=ident[:])
+            return tp
+
+        def evacuate(on_vector, tp, grp, b):
+            dst = grp[:].bitcast(F32)[:, b * 512:(b + 1) * 512].rearrange("p (g c u) -> p g c u", g=2, u=2)
+            src = tp[:].rearrange("p (g u c) -> p g c u", g=2, u=2)
+            if on_vector:
+                nc.vector.tensor_copy(out=dst, in_=src)
+            else:
+                nc.scalar.copy(out=dst, in_=src)
+
+        def xh_job(half, extra=None):
+            grp = grpp.tile([P, 4096], BF16, name="grp", align_bytes=64)
+            for b in range(4):
+                s = half * 4 + b
+                srcs = [xf[:, s * 256:s * 256 + 128], xf[:, s * 256 + 128:s * 256 + 256],
+                        hf[:, s * 256:s * 256 + 128], hf[:, s * 256 + 128:s * 256 + 256]]
+                tp = transpose_bank(srcs)
+                evacuate(b % 2 == 0, tp, grp, b)
+            if extra is not None:
+                extra()
+            cols = slice(half * 1024, (half + 1) * 1024)
+            nc.vector.quantize_mx(out=x_codes[:, cols].bitcast(FP8X4), scales=x_scales[:, cols], in_=grp[:])
+
+        def bias_setup():
+            nc.vector.tensor_copy(out=b_f32[:].rearrange("r (t p) -> r t p", t=4),
+                                  in_=b_rows[:].rearrange("r (p t) -> r t p", t=4))
+            bt = ps_tb.tile([P, 512], F32, name="tb")
+            for t in range(4):
+                nc.tensor.transpose(out=bt[:, t * P:(t + 1) * P], in_=b_f32[:, t * P:(t + 1) * P], identity=ident[:])
+            nc.vector.tensor_copy(out=bias_sb[:].rearrange("p (t r) -> p t r", t=4),
+                                  in_=bt[:].rearrange("p (t r) -> p t r", t=4)[:, :, 0:24])
+
+        codes = {}
+        scales = {}
+        grps = {}
+        accs = {}
+        gate_sb = {}
+        ft = {}
+        mt = {}
+        m2 = {}
+        fc = {}
+
+        def vector_takes(j, b):
+            return b == 0 or (b == 2 and j % 6 == 0)
+
+        def teq_front(j):
+            rawf = raw[j][:].bitcast(F32)
+            grp = grpp.tile([P, 4096], BF16, name="grp", align_bytes=64)
+            grps[j] = grp
+            for b in range(4):
+                tp = transpose_bank([rawf[:, (4 * b + q) * P:(4 * b + q + 1) * P] for q in range(4)])
+                evacuate(vector_takes(j, b), tp, grp, b)
+
+        def quantise(j):
+            cd = codep.tile([P, 1024], U32, name="cd", align_bytes=64)
+            sc = codep.tile([P, 1024], U8, name="sc", align_bytes=64)
+            nc.vector.quantize_mx(out=cd[:].bitcast(FP8X4), scales=sc[:], in_=grps[j][:])
+            codes[j] = cd
+            scales[j] = sc
+
+        def multiply(j):
+            s = j // GATES
+            acc = ps_acc.tile([P, 512], F32, name="acc")
+            accs[j] = acc
+            for t in range(4):
+                for g2 in range(2):
+                    wc = slice((2 * t + g2) * P, (2 * t + g2 + 1) * P)
+                    xc = slice((2 * s + g2) * P, (2 * s + g2 + 1) * P)
+                    nc.tensor.matmul_mx(out=acc[:, t * P:(t + 1) * P],
+                                        lhsT=codes[j][:, wc].bitcast(FP8X4), lhsT_scale=scales[j][:, wc],
+                                        rhs=x_codes[:, xc].bitcast(FP8X4), rhs_scale=x_scales[:, xc],
+                                        start=(g2 == 0), stop=(g2 == 1))
+
+        def activate(j):
+            s, g = divmod(j, GATES)
+            gt = gatep.tile([P, 512], F32, name="gate%d" % g)
+            gate_sb[j] = gt
+            for t in range(4):
+                idx = t * 24 + g * 8 + s
+                nc.scalar.activation(out=gt[:, t * P:(t + 1) * P], in_=accs[j][:, t * P:(t + 1) * P],
+                                     func=funcs[g], bias=bias_sb[:, idx:idx + 1])
+
+        def transpose_back(src):
+            tb = ps_tb.tile([P, 512], F32, name="tb")
+            for t in range(4):
+                nc.tensor.transpose(out=tb[:, t * P:(t + 1) * P], in_=src[:, t * P:(t + 1) * P], identity=ident[:])
+            return tb
+
+        def step(j):
+            if j >= 5 and (j - 5) % 3 == 0:
+                s = (j - 5) // 3
+                mt[s] = transpose_back(m2[s])
+            if j < UNITS:
+                teq_front(j)
+            if j >= 3 and (j - 3) % 3 == 0:
+                s = (j - 3) // 3
+                ft[s] = transpose_back(gate_sb[3 * s + 1])
+            if 1 <= j <= UNITS:
+                multiply(j - 1)
+            if j >= 4 and (j - 4) % 3 == 0:
+                s = (j - 4) // 3
+                fc[s] = gatep.tile([P, 512], F32, name="fc")
+                nc.vector.tensor_tensor(out=fc[s][:].rearrange("n (p t) -> n p t", t=4),
+                                        in0=ft[s][:].rearrange("n (t p) -> n p t", t=4),
+                                        in1=c_sb[:, s * 512:(s + 1) * 512].rearrange("n (p t) -> n p t", t=4),
+                                        op=ALU.mult)
+                m2[s] = gatep.tile([P, 512], F32, name="m2")
+                nc.vector.tensor_tensor(out=m2[s][:], in0=gate_sb[3 * s][:], in1=gate_sb[3 * s + 2][:], op=ALU.mult)
+            if j >= 5 and (j - 5) % 3 == 0:
+                s = (j - 5) // 3
+                nc.vector.tensor_tensor(out=o_sb[:, s * 512:(s + 1) * 512].rearrange("n (p t) -> n p t", t=4),
+                                        in0=mt[s][:].rearrange("n (t p) -> n p t", t=4),
+                                        in1=fc[s][:].rearrange("n (p t) -> n p t", t=4),
+                                        op=ALU.add)
+            if j < UNITS:
+                quantise(j)
+            if 1 <= j <= UNITS:
+                activate(j - 1)
+            if j + RAW_BUFS < UNITS:
+                load_w(j + RAW_BUFS)
+
+        xh_job(0, bias_setup)
+        for j in range(UNITS + 3):
+            if j == 6:
+                xh_job(1)
+            step(j)
+        for s in range(STREAMS):
+            nc.sync.dma_start(out=out[:, s * 512:(s + 1) * 512], in_=o_sb[:, s * 512:(s + 1) * 512])

@@ -19,6 +19,13 @@ GATES = 3
 UNITS = STREAMS * GATES
 FLOPS = 2 * 128 * STREAMS * GATES * 512 * 1024
 RAW_BUFS = 12
+LM = 3
+LA = 3
+L_TBF = 5
+L_F1 = 6
+L_G = 6
+L_TBM = 7
+L_F2 = 8
 
 
 def tile_flatlstm_pa_kernel(tc, modulation, h0, c0, Wi, b_i, Wf, b_f, Wg, b_g, out):
@@ -30,7 +37,7 @@ def tile_flatlstm_pa_kernel(tc, modulation, h0, c0, Wi, b_i, Wf, b_f, Wg, b_g, o
         const = ctx.enter_context(tc.tile_pool(name="const", bufs=1))
         rawp = ctx.enter_context(tc.tile_pool(name="rawp", bufs=RAW_BUFS))
         grpp = ctx.enter_context(tc.tile_pool(name="grpp", bufs=3))
-        codep = ctx.enter_context(tc.tile_pool(name="codep", bufs=3))
+        codep = ctx.enter_context(tc.tile_pool(name="codep", bufs=4))
         gatep = ctx.enter_context(tc.tile_pool(name="gatep", bufs=2))
         ps_tp = ctx.enter_context(tc.psum_pool(name="ps_tp", bufs=4))
         ps_acc = ctx.enter_context(tc.psum_pool(name="ps_acc", bufs=2))
@@ -129,7 +136,7 @@ def tile_flatlstm_pa_kernel(tc, modulation, h0, c0, Wi, b_i, Wf, b_f, Wg, b_g, o
         fc = {}
 
         def vector_takes(j, b):
-            return b == 0 or (b == 2 and j % 6 == 0)
+            return b == 3
 
         def teq_front(j):
             rawf = raw[j][:].bitcast(F32)
@@ -174,41 +181,56 @@ def tile_flatlstm_pa_kernel(tc, modulation, h0, c0, Wi, b_i, Wf, b_f, Wg, b_g, o
                 nc.tensor.transpose(out=tb[:, t * P:(t + 1) * P], in_=src[:, t * P:(t + 1) * P], identity=ident[:])
             return tb
 
+        def f_times_c(s):
+            fc[s] = gatep.tile([P, 512], F32, name="fc")
+            nc.vector.tensor_tensor(out=fc[s][:].rearrange("n (p t) -> n p t", t=4),
+                                    in0=ft[s][:].rearrange("n (t p) -> n p t", t=4),
+                                    in1=c_sb[:, s * 512:(s + 1) * 512].rearrange("n (p t) -> n p t", t=4),
+                                    op=ALU.mult)
+
+        def i_times_g(s):
+            m2[s] = gatep.tile([P, 512], F32, name="m2")
+            nc.vector.tensor_tensor(out=m2[s][:], in0=gate_sb[3 * s][:], in1=gate_sb[3 * s + 2][:], op=ALU.mult)
+
+        def final_add(s):
+            nc.vector.tensor_tensor(out=o_sb[:, s * 512:(s + 1) * 512].rearrange("n (p t) -> n p t", t=4),
+                                    in0=mt[s][:].rearrange("n (t p) -> n p t", t=4),
+                                    in1=fc[s][:].rearrange("n (p t) -> n p t", t=4),
+                                    op=ALU.add)
+
+        def due(j, first):
+            s, r = divmod(j - first, 3)
+            return s if (r == 0 and 0 <= s < STREAMS) else None
+
         def step(j):
-            if j >= 5 and (j - 5) % 3 == 0:
-                s = (j - 5) // 3
-                mt[s] = transpose_back(m2[s])
+            if 0 <= j - LM < UNITS:
+                multiply(j - LM)
+            if 0 <= j - 1 < UNITS:
+                quantise(j - 1)
             if j < UNITS:
                 teq_front(j)
-            if j >= 3 and (j - 3) % 3 == 0:
-                s = (j - 3) // 3
+            s = due(j, L_TBF)
+            if s is not None:
                 ft[s] = transpose_back(gate_sb[3 * s + 1])
-            if 1 <= j <= UNITS:
-                multiply(j - 1)
-            if j >= 4 and (j - 4) % 3 == 0:
-                s = (j - 4) // 3
-                fc[s] = gatep.tile([P, 512], F32, name="fc")
-                nc.vector.tensor_tensor(out=fc[s][:].rearrange("n (p t) -> n p t", t=4),
-                                        in0=ft[s][:].rearrange("n (t p) -> n p t", t=4),
-                                        in1=c_sb[:, s * 512:(s + 1) * 512].rearrange("n (p t) -> n p t", t=4),
-                                        op=ALU.mult)
-                m2[s] = gatep.tile([P, 512], F32, name="m2")
-                nc.vector.tensor_tensor(out=m2[s][:], in0=gate_sb[3 * s][:], in1=gate_sb[3 * s + 2][:], op=ALU.mult)
-            if j >= 5 and (j - 5) % 3 == 0:
-                s = (j - 5) // 3
-                nc.vector.tensor_tensor(out=o_sb[:, s * 512:(s + 1) * 512].rearrange("n (p t) -> n p t", t=4),
-                                        in0=mt[s][:].rearrange("n (t p) -> n p t", t=4),
-                                        in1=fc[s][:].rearrange("n (p t) -> n p t", t=4),
-                                        op=ALU.add)
-            if j < UNITS:
-                quantise(j)
-            if 1 <= j <= UNITS:
-                activate(j - 1)
+            s = due(j, L_TBM)
+            if s is not None:
+                mt[s] = transpose_back(m2[s])
+            if 0 <= j - LA < UNITS:
+                activate(j - LA)
+            s = due(j, L_F1)
+            if s is not None:
+                f_times_c(s)
+            s = due(j, L_G)
+            if s is not None:
+                i_times_g(s)
+            s = due(j, L_F2)
+            if s is not None:
+                final_add(s)
             if j + RAW_BUFS < UNITS:
                 load_w(j + RAW_BUFS)
 
         xh_job(0, bias_setup)
-        for j in range(UNITS + 3):
+        for j in range(UNITS + L_F2):
             if j == 6:
                 xh_job(1)
             step(j)

@@ -1,8 +1,6 @@
 from contextlib import ExitStack
 
-import concourse.bass as bass
 import concourse.mybir as mybir
-import concourse.tile as tile
 from concourse.masks import make_identity
 
 F32 = mybir.dt.float32
@@ -17,15 +15,24 @@ P = 128
 STREAMS = 8
 GATES = 3
 UNITS = STREAMS * GATES
+XJOB = UNITS
 FLOPS = 2 * 128 * STREAMS * GATES * 512 * 1024
-RAW_BUFS = 12
+
+RAW_BUFS = 10
+GRP_BUFS = 3
+CODE_BUFS = 6
+GATE_BUFS = 3
+TP_BUFS = 4
+ACC_BUFS = 2
+TB_BUFS = 2
 LM = 3
-LA = 3
-L_TBF = 5
-L_F1 = 6
-L_G = 6
-L_TBM = 7
-L_F2 = 8
+HOLD = 22
+X_AT = (1, 9)
+C_AT = 9
+G_ON_POOL = False
+V_BANK = 3
+EXTRA_V = ()
+V_SET = frozenset([(24, 2), (1, 2), (2, 1), (3, 2), (4, 3), (5, 1), (5, 3), (6, 3), (7, 2), (8, 3), (25, 3), (11, 3), (12, 2), (13, 2), (15, 0), (15, 3), (16, 3), (18, 0), (19, 0), (20, 3), (21, 2), (23, 0), (23, 3)])
 
 
 def tile_flatlstm_pa_kernel(tc, modulation, h0, c0, Wi, b_i, Wf, b_f, Wg, b_g, out):
@@ -36,12 +43,12 @@ def tile_flatlstm_pa_kernel(tc, modulation, h0, c0, Wi, b_i, Wf, b_f, Wg, b_g, o
     with ExitStack() as ctx:
         const = ctx.enter_context(tc.tile_pool(name="const", bufs=1))
         rawp = ctx.enter_context(tc.tile_pool(name="rawp", bufs=RAW_BUFS))
-        grpp = ctx.enter_context(tc.tile_pool(name="grpp", bufs=3))
-        codep = ctx.enter_context(tc.tile_pool(name="codep", bufs=4))
-        gatep = ctx.enter_context(tc.tile_pool(name="gatep", bufs=2))
-        ps_tp = ctx.enter_context(tc.psum_pool(name="ps_tp", bufs=4))
-        ps_acc = ctx.enter_context(tc.psum_pool(name="ps_acc", bufs=2))
-        ps_tb = ctx.enter_context(tc.psum_pool(name="ps_tb", bufs=2))
+        grpp = ctx.enter_context(tc.tile_pool(name="grpp", bufs=GRP_BUFS))
+        codep = ctx.enter_context(tc.tile_pool(name="codep", bufs=CODE_BUFS))
+        gatep = ctx.enter_context(tc.tile_pool(name="gatep", bufs=GATE_BUFS))
+        ps_tp = ctx.enter_context(tc.psum_pool(name="ps_tp", bufs=TP_BUFS))
+        ps_acc = ctx.enter_context(tc.psum_pool(name="ps_acc", bufs=ACC_BUFS))
+        ps_tb = ctx.enter_context(tc.psum_pool(name="ps_tb", bufs=TB_BUFS))
         ctx.enter_context(tc.manual_schedule())
 
         ident = const.tile([P, P], F32, name="ident")
@@ -55,22 +62,194 @@ def tile_flatlstm_pa_kernel(tc, modulation, h0, c0, Wi, b_i, Wf, b_f, Wg, b_g, o
         b_f32 = const.tile([P, 512], F32, name="b_f32")
         bias_sb = const.tile([P, 4 * 24], F32, name="bias_sb")
         warm = const.tile([P, 2], F32, name="warm")
-
         xf = x_sb[:].bitcast(F32)
         hf = h_sb[:].bitcast(F32)
 
-        raw = {}
+        live = {}
 
-        def load_w(u):
-            s, g = divmod(u, GATES)
-            t = rawp.tile([P, 4096], BF16, name="raw")
-            nc.sync.dma_start(out=t[:], in_=weights[g][s].rearrange("(p t) d -> p (t d)", t=4))
-            raw[u] = t
+        def on_vector(job, b):
+            return (job, b) in V_SET
 
-        def load_xh(half):
-            cols = slice(half * 2048, (half + 1) * 2048)
-            nc.sync.dma_start(out=x_sb[:, cols], in_=modulation[:, cols])
-            nc.sync.dma_start(out=h_sb[:, cols], in_=h0[:, cols])
+        def emit(op):
+            kind = op[0]
+            k = op[1]
+            if kind == "LW":
+                s, g = divmod(k, GATES)
+                piece, pieces = op[2], op[3]
+                if piece == 0:
+                    live["raw", k] = rawp.tile([P, 4096], BF16, name="raw")
+                w = 4096 // pieces
+                cols = slice(piece * w, (piece + 1) * w)
+                nc.sync.dma_start(out=live["raw", k][:, cols],
+                                  in_=weights[g][s].rearrange("(p t) d -> p (t d)", t=4)[:, cols])
+            elif kind == "LX":
+                cols = slice(k * 2048, (k + 1) * 2048)
+                nc.sync.dma_start(out=x_sb[:, cols], in_=modulation[:, cols])
+                nc.sync.dma_start(out=h_sb[:, cols], in_=h0[:, cols])
+            elif kind == "LC":
+                nc.sync.dma_start(out=c_sb[:], in_=c0)
+            elif kind == "T":
+                b = op[2]
+                if b == 0:
+                    live["grp", k] = grpp.tile([P, 4096], BF16, name="grp", align_bytes=64)
+                if k >= XJOB:
+                    s = (k - XJOB) * 4 + b
+                    srcs = [xf[:, s * 256:s * 256 + 128], xf[:, s * 256 + 128:s * 256 + 256],
+                            hf[:, s * 256:s * 256 + 128], hf[:, s * 256 + 128:s * 256 + 256]]
+                else:
+                    rawf = live["raw", k][:].bitcast(F32)
+                    srcs = [rawf[:, (4 * b + q) * P:(4 * b + q + 1) * P] for q in range(4)]
+                tp = ps_tp.tile([P, 512], F32, name="tp")
+                live["tp", k, b] = tp
+                for q in range(4):
+                    nc.tensor.transpose(out=tp[:, q * P:(q + 1) * P], in_=srcs[q], identity=ident[:])
+            elif kind == "E":
+                b = op[2]
+                dst = live["grp", k][:].bitcast(F32)[:, b * 512:(b + 1) * 512].rearrange(
+                    "p (g c u) -> p g c u", g=2, u=2)
+                src = live["tp", k, b][:].rearrange("p (g u c) -> p g c u", g=2, u=2)
+                if on_vector(k, b):
+                    nc.vector.tensor_copy(out=dst, in_=src)
+                else:
+                    nc.scalar.copy(out=dst, in_=src)
+            elif kind == "Q":
+                if k >= XJOB:
+                    cols = slice((k - XJOB) * 1024, (k - XJOB + 1) * 1024)
+                    cd, sc = x_codes[:, cols], x_scales[:, cols]
+                else:
+                    live["cd", k] = codep.tile([P, 1024], U32, name="cd", align_bytes=64)
+                    live["sc", k] = codep.tile([P, 1024], U8, name="sc", align_bytes=64)
+                    cd, sc = live["cd", k][:], live["sc", k][:]
+                nc.vector.quantize_mx(out=cd.bitcast(FP8X4), scales=sc, in_=live["grp", k][:])
+            elif kind == "M":
+                s = k // GATES
+                acc = ps_acc.tile([P, 512], F32, name="acc")
+                live["acc", k] = acc
+                for t in range(4):
+                    for g2 in range(2):
+                        wc = slice((2 * t + g2) * P, (2 * t + g2 + 1) * P)
+                        xc = slice((2 * s + g2) * P, (2 * s + g2 + 1) * P)
+                        nc.tensor.matmul_mx(out=acc[:, t * P:(t + 1) * P],
+                                            lhsT=live["cd", k][:, wc].bitcast(FP8X4), lhsT_scale=live["sc", k][:, wc],
+                                            rhs=x_codes[:, xc].bitcast(FP8X4), rhs_scale=x_scales[:, xc],
+                                            start=(g2 == 0), stop=(g2 == 1))
+            elif kind == "A":
+                s, g = divmod(k, GATES)
+                gt = gatep.tile([P, 512], F32, name="gate%d" % g)
+                live["gate", k] = gt
+                for t in range(4):
+                    idx = t * 24 + g * 8 + s
+                    nc.scalar.activation(out=gt[:, t * P:(t + 1) * P], in_=live["acc", k][:, t * P:(t + 1) * P],
+                                         func=funcs[g], bias=bias_sb[:, idx:idx + 1])
+            elif kind in ("TF", "TM"):
+                src = live["gate", 3 * k + 1] if kind == "TF" else live["m2", k]
+                tb = ps_tb.tile([P, 512], F32, name="tb")
+                live[kind, k] = tb
+                for t in range(4):
+                    nc.tensor.transpose(out=tb[:, t * P:(t + 1) * P], in_=src[:, t * P:(t + 1) * P], identity=ident[:])
+            elif kind == "F1":
+                live["fc", k] = gatep.tile([P, 512], F32, name="fc")
+                nc.vector.tensor_tensor(out=live["fc", k][:].rearrange("n (p t) -> n p t", t=4),
+                                        in0=live["TF", k][:].rearrange("n (t p) -> n p t", t=4),
+                                        in1=c_sb[:, k * 512:(k + 1) * 512].rearrange("n (p t) -> n p t", t=4),
+                                        op=ALU.mult)
+            elif kind == "G":
+                live["m2", k] = gatep.tile([P, 512], F32, name="m2")
+                eng = nc.gpsimd if G_ON_POOL else nc.vector
+                eng.tensor_tensor(out=live["m2", k][:], in0=live["gate", 3 * k][:], in1=live["gate", 3 * k + 2][:],
+                                  op=ALU.mult)
+            elif kind == "F2":
+                nc.vector.tensor_tensor(out=o_sb[:, k * 512:(k + 1) * 512].rearrange("n (p t) -> n p t", t=4),
+                                        in0=live["TM", k][:].rearrange("n (t p) -> n p t", t=4),
+                                        in1=live["fc", k][:].rearrange("n (p t) -> n p t", t=4),
+                                        op=ALU.add)
+            elif kind == "ST":
+                nc.sync.dma_start(out=out[:, k * 512:(k + 1) * 512], in_=o_sb[:, k * 512:(k + 1) * 512])
+            elif kind == "B0":
+                nc.vector.tensor_copy(out=b_f32[:].rearrange("r (t p) -> r t p", t=4),
+                                      in_=b_rows[:].rearrange("r (p t) -> r t p", t=4))
+            elif kind == "B1":
+                bt = ps_tb.tile([P, 512], F32, name="tb")
+                live["bt", 0] = bt
+                for t in range(4):
+                    nc.tensor.transpose(out=bt[:, t * P:(t + 1) * P], in_=b_f32[:, t * P:(t + 1) * P], identity=ident[:])
+            else:
+                nc.vector.tensor_copy(out=bias_sb[:].rearrange("p (t r) -> p t r", t=4),
+                                      in_=live["bt", 0][:].rearrange("p (t r) -> p t r", t=4)[:, :, 0:24])
+
+        jobs = []
+        for u in range(UNITS):
+            for i in range(2):
+                if X_AT[i] == u:
+                    jobs.append(XJOB + i)
+            jobs.append(u)
+
+        q_sync = []
+        for job in jobs:
+            if job == C_AT:
+                q_sync.append(("LC", 0))
+            if job >= XJOB:
+                q_sync.append(("LX", job - XJOB))
+            else:
+                pieces = 4 if job == 0 else 1
+                q_sync.extend([("LW", job, i, pieces) for i in range(pieces)])
+        q_sync.extend([("ST", s) for s in range(STREAMS)])
+
+        q_pe = [("T", 0, 0), ("T", 0, 1), ("B1", 0), ("T", 0, 2), ("T", 0, 3), ("T", 24, 0), ("T", 24, 1), ("T", 24, 2), ("T", 24, 3), ("T", 1, 0), ("T", 1, 1), ("T", 1, 2), ("T", 1, 3), ("M", 0), ("T", 2, 0), ("T", 2, 1), ("T", 2, 2), ("T", 2, 3), ("M", 1), ("T", 3, 0), ("T", 3, 1), ("T", 3, 2), ("T", 3, 3), ("TF", 0), ("T", 4, 0), ("T", 4, 1), ("T", 4, 2), ("T", 4, 3), ("M", 2), ("M", 3), ("T", 5, 0), ("T", 5, 1), ("T", 5, 2), ("T", 5, 3), ("TM", 0), ("T", 6, 0), ("T", 6, 1), ("T", 6, 2), ("T", 6, 3), ("T", 7, 0), ("T", 7, 1), ("M", 4), ("M", 5), ("T", 7, 2), ("T", 7, 3), ("T", 8, 0), ("T", 8, 1), ("T", 8, 2), ("T", 8, 3), ("T", 25, 0), ("M", 6), ("M", 7), ("T", 25, 1), ("T", 25, 2), ("T", 25, 3), ("M", 8), ("TF", 1), ("T", 9, 0), ("T", 9, 1), ("T", 9, 2), ("T", 9, 3), ("TM", 1), ("TF", 2), ("T", 10, 0), ("T", 10, 1), ("T", 10, 2), ("T", 10, 3), ("TM", 2), ("T", 11, 0), ("T", 11, 1), ("T", 11, 2), ("T", 11, 3), ("M", 9), ("T", 12, 0), ("T", 12, 1), ("T", 12, 2), ("T", 12, 3), ("M", 10), ("M", 11), ("T", 13, 0), ("T", 13, 1), ("T", 13, 2), ("T", 13, 3), ("TF", 3), ("T", 14, 0), ("TM", 3), ("T", 14, 1), ("T", 14, 2), ("T", 14, 3), ("T", 15, 0), ("T", 15, 1), ("T", 15, 2), ("M", 12), ("M", 13), ("T", 15, 3), ("T", 16, 0), ("T", 16, 1), ("T", 16, 2), ("T", 16, 3), ("T", 17, 0), ("TF", 4), ("T", 17, 1), ("T", 17, 2), ("T", 17, 3), ("T", 18, 0), ("T", 18, 1), ("T", 18, 2), ("M", 14), ("M", 15), ("T", 18, 3), ("T", 19, 0), ("T", 19, 1), ("T", 19, 2), ("TM", 4), ("T", 19, 3), ("T", 20, 0), ("T", 20, 1), ("T", 20, 2), ("T", 20, 3), ("M", 16), ("M", 17), ("T", 21, 0), ("T", 21, 1), ("T", 21, 2), ("T", 21, 3), ("TF", 5), ("T", 22, 0), ("TM", 5), ("T", 22, 1), ("T", 22, 2), ("T", 22, 3), ("T", 23, 0), ("T", 23, 1), ("T", 23, 2), ("M", 18), ("M", 19), ("T", 23, 3), ("M", 20), ("M", 21), ("TF", 6), ("M", 22), ("M", 23), ("TM", 6), ("TF", 7), ("TM", 7)]
+        q_s = [("E", 0, 0), ("E", 0, 1), ("E", 0, 2), ("E", 0, 3), ("E", 24, 0), ("E", 24, 1), ("E", 24, 3), ("E", 1, 0), ("E", 1, 1), ("E", 1, 3), ("A", 0), ("E", 2, 0), ("E", 2, 2), ("E", 2, 3), ("A", 1), ("E", 3, 0), ("E", 3, 1), ("E", 3, 3), ("E", 4, 0), ("E", 4, 1), ("E", 4, 2), ("A", 2), ("A", 3), ("E", 5, 0), ("E", 5, 2), ("E", 6, 0), ("E", 6, 1), ("E", 6, 2), ("E", 7, 0), ("E", 7, 1), ("A", 4), ("A", 5), ("E", 7, 3), ("E", 8, 0), ("E", 8, 1), ("E", 8, 2), ("E", 25, 0), ("A", 6), ("A", 7), ("E", 25, 1), ("E", 25, 2), ("A", 8), ("E", 9, 0), ("E", 9, 1), ("E", 9, 2), ("E", 9, 3), ("E", 10, 0), ("E", 10, 1), ("E", 10, 2), ("E", 10, 3), ("E", 11, 0), ("E", 11, 1), ("E", 11, 2), ("A", 9), ("E", 12, 0), ("E", 12, 1), ("E", 12, 3), ("A", 10), ("A", 11), ("E", 13, 0), ("E", 13, 1), ("E", 13, 3), ("E", 14, 0), ("E", 14, 1), ("E", 14, 2), ("E", 14, 3), ("E", 15, 1), ("E", 15, 2), ("A", 12), ("A", 13), ("E", 16, 0), ("E", 16, 1), ("E", 16, 2), ("E", 17, 0), ("E", 17, 1), ("E", 17, 2), ("E", 17, 3), ("E", 18, 1), ("E", 18, 2), ("A", 14), ("A", 15), ("E", 18, 3), ("E", 19, 1), ("E", 19, 2), ("E", 19, 3), ("E", 20, 0), ("E", 20, 1), ("E", 20, 2), ("A", 16), ("A", 17), ("E", 21, 0), ("E", 21, 1), ("E", 21, 3), ("E", 22, 0), ("E", 22, 1), ("E", 22, 2), ("E", 22, 3), ("E", 23, 1), ("E", 23, 2), ("A", 18), ("A", 19), ("A", 20), ("A", 21), ("A", 22), ("A", 23)]
+        q_v = [("B0", 0), ("B2", 0), ("Q", 0), ("E", 24, 2), ("Q", 24), ("E", 1, 2), ("Q", 1), ("E", 2, 1), ("Q", 2), ("E", 3, 2), ("Q", 3), ("E", 4, 3), ("Q", 4), ("G", 0), ("E", 5, 1), ("E", 5, 3), ("Q", 5), ("E", 6, 3), ("Q", 6), ("E", 7, 2), ("G", 1), ("Q", 7), ("E", 8, 3), ("Q", 8), ("F1", 0), ("F2", 0), ("E", 25, 3), ("Q", 25), ("F1", 1), ("G", 2), ("F2", 1), ("F1", 2), ("Q", 9), ("F2", 2), ("Q", 10), ("E", 11, 3), ("Q", 11), ("E", 12, 2), ("Q", 12), ("G", 3), ("E", 13, 2), ("F1", 3), ("Q", 13), ("F2", 3), ("E", 15, 0), ("Q", 14), ("E", 15, 3), ("Q", 15), ("E", 16, 3), ("F1", 4), ("Q", 16), ("E", 18, 0), ("Q", 17), ("G", 4), ("E", 19, 0), ("Q", 18), ("F2", 4), ("Q", 19), ("E", 20, 3), ("Q", 20), ("G", 5), ("E", 21, 2), ("F1", 5), ("Q", 21), ("F2", 5), ("E", 23, 0), ("Q", 22), ("E", 23, 3), ("Q", 23), ("G", 6), ("F1", 6), ("F2", 6), ("F1", 7), ("G", 7), ("F2", 7)]
+        q_g = []
+        queues = [q_sync, q_pe, q_s, q_v, q_g]
+
+        needs = {}
+
+        def need(op, other):
+            needs[op] = needs.get(op, []) + [other]
+
+        def ring(allocs, bufs, users):
+            for i in range(bufs, len(allocs)):
+                for other in users(allocs[i - bufs]):
+                    need(allocs[i], other)
+
+        for job in jobs:
+            for b in range(4):
+                if job >= XJOB:
+                    need(("T", job, b), ("LX", job - XJOB))
+                elif job == 0:
+                    need(("T", job, b), ("LW", 0, b, 4))
+                else:
+                    need(("T", job, b), ("LW", job, 0, 1))
+                need(("E", job, b), ("T", job, b))
+                need(("Q", job), ("E", job, b))
+        for u in range(UNITS):
+            need(("M", u), ("Q", u))
+            need(("M", u), ("Q", XJOB + u // 12))
+            need(("A", u), ("M", u))
+            need(("A", u), ("B2", 0))
+        need(("B1", 0), ("B0", 0))
+        need(("B2", 0), ("B1", 0))
+        for s in range(STREAMS):
+            need(("TF", s), ("A", 3 * s + 1))
+            need(("F1", s), ("TF", s))
+            need(("F1", s), ("LC", 0))
+            need(("G", s), ("A", 3 * s))
+            need(("G", s), ("A", 3 * s + 2))
+            need(("TM", s), ("G", s))
+            need(("F2", s), ("TM", s))
+            need(("F2", s), ("F1", s))
+            need(("ST", s), ("F2", s))
+        ring([op for op in q_sync if op[0] == "LW" and op[2] == 0], RAW_BUFS, lambda o: [("T", o[1], 3)])
+        ring([op for op in q_pe if op[0] == "T"], TP_BUFS, lambda o: [("E", o[1], o[2])])
+        ring([op for op in q_pe if op[0] == "T" and op[2] == 0], GRP_BUFS, lambda o: [("Q", o[1])])
+        ring([op for op in q_v if op[0] == "Q" and op[1] < XJOB], CODE_BUFS, lambda o: [("M", o[1])])
+        ring([op for op in q_pe if op[0] == "M"], ACC_BUFS, lambda o: [("A", o[1])])
+        ring([op for op in q_pe if op[0] in ("B1", "TF", "TM")], TB_BUFS,
+             lambda o: [{"B1": ("B2", 0), "TF": ("F1", o[1]), "TM": ("F2", o[1])}[o[0]]])
+        ring([("A", 3 * s) for s in range(STREAMS)], GATE_BUFS, lambda o: [("G", o[1] // 3)])
+        ring([("A", 3 * s + 1) for s in range(STREAMS)], GATE_BUFS, lambda o: [("TF", o[1] // 3)])
+        ring([("A", 3 * s + 2) for s in range(STREAMS)], GATE_BUFS, lambda o: [("G", o[1] // 3)])
+        ring([("F1", s) for s in range(STREAMS)], GATE_BUFS, lambda o: [("F2", o[1])])
+        ring([("G", s) for s in range(STREAMS)], GATE_BUFS, lambda o: [("TM", o[1])])
 
         nc.vector.memset(warm[:], 0.0)
         nc.vector.memset(b_rows[:], 0.0)
@@ -79,160 +258,16 @@ def tile_flatlstm_pa_kernel(tc, modulation, h0, c0, Wi, b_i, Wf, b_f, Wg, b_g, o
         nc.scalar.activation(out=warm[:, 1:2], in_=warm[:, 0:1], func=ACT.Sigmoid)
         make_identity(nc, ident[:])
 
-        load_xh(0)
-        for u in range(3):
-            load_w(u)
-        nc.sync.dma_start(out=c_sb[:], in_=c0)
-        for u in range(3, 6):
-            load_w(u)
-        load_xh(1)
-        for u in range(6, RAW_BUFS):
-            load_w(u)
-
-        def transpose_bank(srcs):
-            tp = ps_tp.tile([P, 512], F32, name="tp")
-            for q in range(4):
-                nc.tensor.transpose(out=tp[:, q * P:(q + 1) * P], in_=srcs[q], identity=ident[:])
-            return tp
-
-        def evacuate(on_vector, tp, grp, b):
-            dst = grp[:].bitcast(F32)[:, b * 512:(b + 1) * 512].rearrange("p (g c u) -> p g c u", g=2, u=2)
-            src = tp[:].rearrange("p (g u c) -> p g c u", g=2, u=2)
-            if on_vector:
-                nc.vector.tensor_copy(out=dst, in_=src)
-            else:
-                nc.scalar.copy(out=dst, in_=src)
-
-        def xh_job(half, extra=None):
-            grp = grpp.tile([P, 4096], BF16, name="grp", align_bytes=64)
-            for b in range(4):
-                s = half * 4 + b
-                srcs = [xf[:, s * 256:s * 256 + 128], xf[:, s * 256 + 128:s * 256 + 256],
-                        hf[:, s * 256:s * 256 + 128], hf[:, s * 256 + 128:s * 256 + 256]]
-                tp = transpose_bank(srcs)
-                evacuate(b % 2 == 0, tp, grp, b)
-            if extra is not None:
-                extra()
-            cols = slice(half * 1024, (half + 1) * 1024)
-            nc.vector.quantize_mx(out=x_codes[:, cols].bitcast(FP8X4), scales=x_scales[:, cols], in_=grp[:])
-
-        def bias_setup():
-            nc.vector.tensor_copy(out=b_f32[:].rearrange("r (t p) -> r t p", t=4),
-                                  in_=b_rows[:].rearrange("r (p t) -> r t p", t=4))
-            bt = ps_tb.tile([P, 512], F32, name="tb")
-            for t in range(4):
-                nc.tensor.transpose(out=bt[:, t * P:(t + 1) * P], in_=b_f32[:, t * P:(t + 1) * P], identity=ident[:])
-            nc.vector.tensor_copy(out=bias_sb[:].rearrange("p (t r) -> p t r", t=4),
-                                  in_=bt[:].rearrange("p (t r) -> p t r", t=4)[:, :, 0:24])
-
-        codes = {}
-        scales = {}
-        grps = {}
-        accs = {}
-        gate_sb = {}
-        ft = {}
-        mt = {}
-        m2 = {}
-        fc = {}
-
-        def vector_takes(j, b):
-            return b == 3
-
-        def teq_front(j):
-            rawf = raw[j][:].bitcast(F32)
-            grp = grpp.tile([P, 4096], BF16, name="grp", align_bytes=64)
-            grps[j] = grp
-            for b in range(4):
-                tp = transpose_bank([rawf[:, (4 * b + q) * P:(4 * b + q + 1) * P] for q in range(4)])
-                evacuate(vector_takes(j, b), tp, grp, b)
-
-        def quantise(j):
-            cd = codep.tile([P, 1024], U32, name="cd", align_bytes=64)
-            sc = codep.tile([P, 1024], U8, name="sc", align_bytes=64)
-            nc.vector.quantize_mx(out=cd[:].bitcast(FP8X4), scales=sc[:], in_=grps[j][:])
-            codes[j] = cd
-            scales[j] = sc
-
-        def multiply(j):
-            s = j // GATES
-            acc = ps_acc.tile([P, 512], F32, name="acc")
-            accs[j] = acc
-            for t in range(4):
-                for g2 in range(2):
-                    wc = slice((2 * t + g2) * P, (2 * t + g2 + 1) * P)
-                    xc = slice((2 * s + g2) * P, (2 * s + g2 + 1) * P)
-                    nc.tensor.matmul_mx(out=acc[:, t * P:(t + 1) * P],
-                                        lhsT=codes[j][:, wc].bitcast(FP8X4), lhsT_scale=scales[j][:, wc],
-                                        rhs=x_codes[:, xc].bitcast(FP8X4), rhs_scale=x_scales[:, xc],
-                                        start=(g2 == 0), stop=(g2 == 1))
-
-        def activate(j):
-            s, g = divmod(j, GATES)
-            gt = gatep.tile([P, 512], F32, name="gate%d" % g)
-            gate_sb[j] = gt
-            for t in range(4):
-                idx = t * 24 + g * 8 + s
-                nc.scalar.activation(out=gt[:, t * P:(t + 1) * P], in_=accs[j][:, t * P:(t + 1) * P],
-                                     func=funcs[g], bias=bias_sb[:, idx:idx + 1])
-
-        def transpose_back(src):
-            tb = ps_tb.tile([P, 512], F32, name="tb")
-            for t in range(4):
-                nc.tensor.transpose(out=tb[:, t * P:(t + 1) * P], in_=src[:, t * P:(t + 1) * P], identity=ident[:])
-            return tb
-
-        def f_times_c(s):
-            fc[s] = gatep.tile([P, 512], F32, name="fc")
-            nc.vector.tensor_tensor(out=fc[s][:].rearrange("n (p t) -> n p t", t=4),
-                                    in0=ft[s][:].rearrange("n (t p) -> n p t", t=4),
-                                    in1=c_sb[:, s * 512:(s + 1) * 512].rearrange("n (p t) -> n p t", t=4),
-                                    op=ALU.mult)
-
-        def i_times_g(s):
-            m2[s] = gatep.tile([P, 512], F32, name="m2")
-            nc.vector.tensor_tensor(out=m2[s][:], in0=gate_sb[3 * s][:], in1=gate_sb[3 * s + 2][:], op=ALU.mult)
-
-        def final_add(s):
-            nc.vector.tensor_tensor(out=o_sb[:, s * 512:(s + 1) * 512].rearrange("n (p t) -> n p t", t=4),
-                                    in0=mt[s][:].rearrange("n (t p) -> n p t", t=4),
-                                    in1=fc[s][:].rearrange("n (p t) -> n p t", t=4),
-                                    op=ALU.add)
-
-        def due(j, first):
-            s, r = divmod(j - first, 3)
-            return s if (r == 0 and 0 <= s < STREAMS) else None
-
-        def step(j):
-            if 0 <= j - LM < UNITS:
-                multiply(j - LM)
-            if 0 <= j - 1 < UNITS:
-                quantise(j - 1)
-            if j < UNITS:
-                teq_front(j)
-            s = due(j, L_TBF)
-            if s is not None:
-                ft[s] = transpose_back(gate_sb[3 * s + 1])
-            s = due(j, L_TBM)
-            if s is not None:
-                mt[s] = transpose_back(m2[s])
-            if 0 <= j - LA < UNITS:
-                activate(j - LA)
-            s = due(j, L_F1)
-            if s is not None:
-                f_times_c(s)
-            s = due(j, L_G)
-            if s is not None:
-                i_times_g(s)
-            s = due(j, L_F2)
-            if s is not None:
-                final_add(s)
-            if j + RAW_BUFS < UNITS:
-                load_w(j + RAW_BUFS)
-
-        xh_job(0, bias_setup)
-        for j in range(UNITS + L_F2):
-            if j == 6:
-                xh_job(1)
-            step(j)
-        for s in range(STREAMS):
-            nc.sync.dma_start(out=out[:, s * 512:(s + 1) * 512], in_=o_sb[:, s * 512:(s + 1) * 512])
+        done = set()
+        heads = [0 for q in queues]
+        left = sum([len(q) for q in queues])
+        while left > 0:
+            moved = 0
+            for i, q in enumerate(queues):
+                while heads[i] < len(q) and all([o in done for o in needs.get(q[heads[i]], [])]):
+                    emit(q[heads[i]])
+                    done.add(q[heads[i]])
+                    heads[i] += 1
+                    moved += 1
+            assert moved > 0, "the queues wait for each other"
+            left -= moved

@@ -13,243 +13,183 @@ ALU = mybir.AluOpType
 
 P = 128
 STREAMS = 8
+WIDTH = 512
 GATES = 3
 UNITS = STREAMS * GATES
-XJOB = UNITS
-FLOPS = 2 * 128 * STREAMS * GATES * 512 * 1024
+FLOPS = 2 * P * UNITS * WIDTH * 2 * WIDTH
 
 RAW_BUFS = 10
-GRP_BUFS = 3
-CODE_BUFS = 6
-GATE_BUFS = 3
-TP_BUFS = 4
-ACC_BUFS = 2
-TB_BUFS = 2
-LM = 3
-HOLD = 22
-X_AT = (1, 9)
-C_AT = 9
-G_ON_POOL = False
-V_BANK = 3
-EXTRA_V = ()
-V_SET = frozenset([(24, 2), (1, 2), (2, 1), (3, 2), (4, 3), (5, 1), (5, 3), (6, 3), (7, 2), (8, 3), (25, 3), (11, 3), (12, 2), (13, 2), (15, 0), (15, 3), (16, 3), (18, 0), (19, 0), (20, 3), (21, 2), (23, 0), (23, 3)])
 
 
 def tile_flatlstm_pa_kernel(tc, modulation, h0, c0, Wi, b_i, Wf, b_f, Wg, b_g, out):
     nc = tc.nc
-    weights = (Wi, Wf, Wg)
-    biases = (b_i, b_f, b_g)
+    weights = (Wf, Wi, Wg)
+    biases = (b_f, b_i, b_g)
     funcs = (ACT.Sigmoid, ACT.Sigmoid, ACT.Tanh)
     with ExitStack() as ctx:
         const = ctx.enter_context(tc.tile_pool(name="const", bufs=1))
         rawp = ctx.enter_context(tc.tile_pool(name="rawp", bufs=RAW_BUFS))
-        grpp = ctx.enter_context(tc.tile_pool(name="grpp", bufs=GRP_BUFS))
-        codep = ctx.enter_context(tc.tile_pool(name="codep", bufs=CODE_BUFS))
-        gatep = ctx.enter_context(tc.tile_pool(name="gatep", bufs=GATE_BUFS))
-        ps_tp = ctx.enter_context(tc.psum_pool(name="ps_tp", bufs=TP_BUFS))
-        ps_acc = ctx.enter_context(tc.psum_pool(name="ps_acc", bufs=ACC_BUFS))
-        ps_tb = ctx.enter_context(tc.psum_pool(name="ps_tb", bufs=TB_BUFS))
+        grpp = ctx.enter_context(tc.tile_pool(name="grpp", bufs=4))
+        xgrpp = ctx.enter_context(tc.tile_pool(name="xgrpp", bufs=2))
+        codep = ctx.enter_context(tc.tile_pool(name="codep", bufs=6))
+        gatep = ctx.enter_context(tc.tile_pool(name="gatep", bufs=3))
+        ps_tp = ctx.enter_context(tc.psum_pool(name="ps_tp", bufs=4))
+        ps_acc = ctx.enter_context(tc.psum_pool(name="ps_acc", bufs=2))
+        ps_tb = ctx.enter_context(tc.psum_pool(name="ps_tb", bufs=2))
         ctx.enter_context(tc.manual_schedule())
 
         ident = const.tile([P, P], F32, name="ident")
-        x_sb = const.tile([P, 4096], BF16, name="x_sb")
-        h_sb = const.tile([P, 4096], BF16, name="h_sb")
-        c_sb = const.tile([P, 4096], BF16, name="c_sb")
-        o_sb = const.tile([P, 4096], F32, name="o_sb")
-        x_codes = const.tile([P, 2048], U32, name="x_codes", align_bytes=64)
-        x_scales = const.tile([P, 2048], U8, name="x_scales", align_bytes=64)
-        b_rows = const.tile([P, 512], BF16, name="b_rows")
-        b_f32 = const.tile([P, 512], F32, name="b_f32")
-        bias_sb = const.tile([P, 4 * 24], F32, name="bias_sb")
+        x_sb = const.tile([P, STREAMS * WIDTH], BF16, name="x_sb")
+        h_sb = const.tile([P, STREAMS * WIDTH], BF16, name="h_sb")
+        c_sb = const.tile([P, STREAMS * WIDTH], BF16, name="c_sb")
+        o_sb = const.tile([P, STREAMS * WIDTH], F32, name="o_sb")
+        x_codes = const.tile([P, STREAMS * 256], U32, name="x_codes", align_bytes=64)
+        x_scales = const.tile([P, STREAMS * 256], U8, name="x_scales", align_bytes=64)
+        b_rows = const.tile([P, WIDTH], BF16, name="b_rows")
+        b_f32 = const.tile([P, WIDTH], F32, name="b_f32")
+        bias_sb = const.tile([P, 4 * UNITS], F32, name="bias_sb")
         warm = const.tile([P, 2], F32, name="warm")
-        xf = x_sb[:].bitcast(F32)
-        hf = h_sb[:].bitcast(F32)
+        x_words = x_sb[:].bitcast(F32)
+        h_words = h_sb[:].bitcast(F32)
 
-        live = {}
+        raw = {}
+        grp = {}
+        codes = {}
+        scales = {}
+        acc = {}
+        gate = {}
+        back = {}
+        fc = {}
+        ig = {}
 
-        def on_vector(job, b):
-            return (job, b) in V_SET
+        def cols_of(s):
+            return slice(s * WIDTH, (s + 1) * WIDTH)
 
-        def emit(op):
-            kind = op[0]
-            k = op[1]
-            if kind == "LW":
-                s, g = divmod(k, GATES)
-                piece, pieces = op[2], op[3]
-                if piece == 0:
-                    live["raw", k] = rawp.tile([P, 4096], BF16, name="raw")
-                w = 4096 // pieces
-                cols = slice(piece * w, (piece + 1) * w)
-                nc.sync.dma_start(out=live["raw", k][:, cols],
+        def load_weight(u, pieces):
+            s, g = divmod(u, GATES)
+            raw[u] = rawp.tile([P, 4096], BF16, name="raw")
+            w = 4096 // pieces
+            for i in range(pieces):
+                cols = slice(i * w, (i + 1) * w)
+                nc.sync.dma_start(out=raw[u][:, cols],
                                   in_=weights[g][s].rearrange("(p t) d -> p (t d)", t=4)[:, cols])
-            elif kind == "LX":
-                cols = slice(k * 2048, (k + 1) * 2048)
-                nc.sync.dma_start(out=x_sb[:, cols], in_=modulation[:, cols])
-                nc.sync.dma_start(out=h_sb[:, cols], in_=h0[:, cols])
-            elif kind == "LC":
-                nc.sync.dma_start(out=c_sb[:], in_=c0)
-            elif kind == "T":
-                b = op[2]
-                if b == 0:
-                    live["grp", k] = grpp.tile([P, 4096], BF16, name="grp", align_bytes=64)
-                if k >= XJOB:
-                    s = (k - XJOB) * 4 + b
-                    srcs = [xf[:, s * 256:s * 256 + 128], xf[:, s * 256 + 128:s * 256 + 256],
-                            hf[:, s * 256:s * 256 + 128], hf[:, s * 256 + 128:s * 256 + 256]]
-                else:
-                    rawf = live["raw", k][:].bitcast(F32)
-                    srcs = [rawf[:, (4 * b + q) * P:(4 * b + q + 1) * P] for q in range(4)]
-                tp = ps_tp.tile([P, 512], F32, name="tp")
-                live["tp", k, b] = tp
-                for q in range(4):
-                    nc.tensor.transpose(out=tp[:, q * P:(q + 1) * P], in_=srcs[q], identity=ident[:])
-            elif kind == "E":
-                b = op[2]
-                dst = live["grp", k][:].bitcast(F32)[:, b * 512:(b + 1) * 512].rearrange(
-                    "p (g c u) -> p g c u", g=2, u=2)
-                src = live["tp", k, b][:].rearrange("p (g u c) -> p g c u", g=2, u=2)
-                if on_vector(k, b):
-                    nc.vector.tensor_copy(out=dst, in_=src)
-                else:
-                    nc.scalar.copy(out=dst, in_=src)
-            elif kind == "Q":
-                if k >= XJOB:
-                    cols = slice((k - XJOB) * 1024, (k - XJOB + 1) * 1024)
-                    cd, sc = x_codes[:, cols], x_scales[:, cols]
-                else:
-                    live["cd", k] = codep.tile([P, 1024], U32, name="cd", align_bytes=64)
-                    live["sc", k] = codep.tile([P, 1024], U8, name="sc", align_bytes=64)
-                    cd, sc = live["cd", k][:], live["sc", k][:]
-                nc.vector.quantize_mx(out=cd.bitcast(FP8X4), scales=sc, in_=live["grp", k][:])
-            elif kind == "M":
-                s = k // GATES
-                acc = ps_acc.tile([P, 512], F32, name="acc")
-                live["acc", k] = acc
-                for t in range(4):
-                    for g2 in range(2):
-                        wc = slice((2 * t + g2) * P, (2 * t + g2 + 1) * P)
-                        xc = slice((2 * s + g2) * P, (2 * s + g2 + 1) * P)
-                        nc.tensor.matmul_mx(out=acc[:, t * P:(t + 1) * P],
-                                            lhsT=live["cd", k][:, wc].bitcast(FP8X4), lhsT_scale=live["sc", k][:, wc],
-                                            rhs=x_codes[:, xc].bitcast(FP8X4), rhs_scale=x_scales[:, xc],
-                                            start=(g2 == 0), stop=(g2 == 1))
-            elif kind == "A":
-                s, g = divmod(k, GATES)
-                gt = gatep.tile([P, 512], F32, name="gate%d" % g)
-                live["gate", k] = gt
-                for t in range(4):
-                    idx = t * 24 + g * 8 + s
-                    nc.scalar.activation(out=gt[:, t * P:(t + 1) * P], in_=live["acc", k][:, t * P:(t + 1) * P],
-                                         func=funcs[g], bias=bias_sb[:, idx:idx + 1])
-            elif kind in ("TF", "TM"):
-                src = live["gate", 3 * k + 1] if kind == "TF" else live["m2", k]
-                tb = ps_tb.tile([P, 512], F32, name="tb")
-                live[kind, k] = tb
-                for t in range(4):
-                    nc.tensor.transpose(out=tb[:, t * P:(t + 1) * P], in_=src[:, t * P:(t + 1) * P], identity=ident[:])
-            elif kind == "F1":
-                live["fc", k] = gatep.tile([P, 512], F32, name="fc")
-                nc.vector.tensor_tensor(out=live["fc", k][:].rearrange("n (p t) -> n p t", t=4),
-                                        in0=live["TF", k][:].rearrange("n (t p) -> n p t", t=4),
-                                        in1=c_sb[:, k * 512:(k + 1) * 512].rearrange("n (p t) -> n p t", t=4),
-                                        op=ALU.mult)
-            elif kind == "G":
-                live["m2", k] = gatep.tile([P, 512], F32, name="m2")
-                eng = nc.gpsimd if G_ON_POOL else nc.vector
-                eng.tensor_tensor(out=live["m2", k][:], in0=live["gate", 3 * k][:], in1=live["gate", 3 * k + 2][:],
-                                  op=ALU.mult)
-            elif kind == "F2":
-                nc.vector.tensor_tensor(out=o_sb[:, k * 512:(k + 1) * 512].rearrange("n (p t) -> n p t", t=4),
-                                        in0=live["TM", k][:].rearrange("n (t p) -> n p t", t=4),
-                                        in1=live["fc", k][:].rearrange("n (p t) -> n p t", t=4),
-                                        op=ALU.add)
-            elif kind == "ST":
-                nc.sync.dma_start(out=out[:, k * 512:(k + 1) * 512], in_=o_sb[:, k * 512:(k + 1) * 512])
-            elif kind == "B0":
-                nc.vector.tensor_copy(out=b_f32[:].rearrange("r (t p) -> r t p", t=4),
-                                      in_=b_rows[:].rearrange("r (p t) -> r t p", t=4))
-            elif kind == "B1":
-                bt = ps_tb.tile([P, 512], F32, name="tb")
-                live["bt", 0] = bt
-                for t in range(4):
-                    nc.tensor.transpose(out=bt[:, t * P:(t + 1) * P], in_=b_f32[:, t * P:(t + 1) * P], identity=ident[:])
+
+        def load_xh(s):
+            nc.sync.dma_start(out=x_sb[:, cols_of(s)], in_=modulation[:, cols_of(s)])
+            nc.sync.dma_start(out=h_sb[:, cols_of(s)], in_=h0[:, cols_of(s)])
+
+        def load_c(s):
+            nc.sync.dma_start(out=c_sb[:, cols_of(s)], in_=c0[:, cols_of(s)])
+
+        def store(s):
+            nc.sync.dma_start(out=out[:, cols_of(s)], in_=o_sb[:, cols_of(s)])
+
+        def turn(srcs):
+            tp = ps_tp.tile([P, 512], F32, name="tp")
+            for q in range(4):
+                nc.tensor.transpose(out=tp[:, q * P:(q + 1) * P], in_=srcs[q], identity=ident[:])
+            return tp
+
+        def pack(dst_tile, b, tp, on_vector):
+            dst = dst_tile[:].bitcast(F32)[:, b * 512:(b + 1) * 512].rearrange("p (g c u) -> p g c u", g=2, u=2)
+            src = tp[:].rearrange("p (g u c) -> p g c u", g=2, u=2)
+            if on_vector:
+                nc.vector.tensor_copy(out=dst, in_=src)
             else:
-                nc.vector.tensor_copy(out=bias_sb[:].rearrange("p (t r) -> p t r", t=4),
-                                      in_=live["bt", 0][:].rearrange("p (t r) -> p t r", t=4)[:, :, 0:24])
+                nc.scalar.copy(out=dst, in_=src)
 
-        jobs = []
-        for u in range(UNITS):
-            for i in range(2):
-                if X_AT[i] == u:
-                    jobs.append(XJOB + i)
-            jobs.append(u)
+        def turn_weight(u, b):
+            if b == 0:
+                grp[u] = grpp.tile([P, 4096], BF16, name="grp", align_bytes=64)
+            words = raw[u][:].bitcast(F32)
+            tp = turn([words[:, (4 * b + q) * P:(4 * b + q + 1) * P] for q in range(4)])
+            pack(grp[u], b, tp, b == 2)
 
-        q_sync = []
-        for job in jobs:
-            if job == C_AT:
-                q_sync.append(("LC", 0))
-            if job >= XJOB:
-                q_sync.append(("LX", job - XJOB))
-            else:
-                pieces = 4 if job == 0 else 1
-                q_sync.extend([("LW", job, i, pieces) for i in range(pieces)])
-        q_sync.extend([("ST", s) for s in range(STREAMS)])
+        def turn_xh(s):
+            grp["x", s] = xgrpp.tile([P, 1024], BF16, name="xgrp", align_bytes=64)
+            lo = slice(s * 256, s * 256 + P)
+            hi = slice(s * 256 + P, (s + 1) * 256)
+            tp = turn([x_words[:, lo], x_words[:, hi], h_words[:, lo], h_words[:, hi]])
+            pack(grp["x", s], 0, tp, False)
 
-        q_pe = [("T", 0, 0), ("T", 0, 1), ("B1", 0), ("T", 0, 2), ("T", 0, 3), ("T", 24, 0), ("T", 24, 1), ("T", 24, 2), ("T", 24, 3), ("T", 1, 0), ("T", 1, 1), ("T", 1, 2), ("T", 1, 3), ("M", 0), ("T", 2, 0), ("T", 2, 1), ("T", 2, 2), ("T", 2, 3), ("M", 1), ("T", 3, 0), ("T", 3, 1), ("T", 3, 2), ("T", 3, 3), ("TF", 0), ("T", 4, 0), ("T", 4, 1), ("T", 4, 2), ("T", 4, 3), ("M", 2), ("M", 3), ("T", 5, 0), ("T", 5, 1), ("T", 5, 2), ("T", 5, 3), ("TM", 0), ("T", 6, 0), ("T", 6, 1), ("T", 6, 2), ("T", 6, 3), ("T", 7, 0), ("T", 7, 1), ("M", 4), ("M", 5), ("T", 7, 2), ("T", 7, 3), ("T", 8, 0), ("T", 8, 1), ("T", 8, 2), ("T", 8, 3), ("T", 25, 0), ("M", 6), ("M", 7), ("T", 25, 1), ("T", 25, 2), ("T", 25, 3), ("M", 8), ("TF", 1), ("T", 9, 0), ("T", 9, 1), ("T", 9, 2), ("T", 9, 3), ("TM", 1), ("TF", 2), ("T", 10, 0), ("T", 10, 1), ("T", 10, 2), ("T", 10, 3), ("TM", 2), ("T", 11, 0), ("T", 11, 1), ("T", 11, 2), ("T", 11, 3), ("M", 9), ("T", 12, 0), ("T", 12, 1), ("T", 12, 2), ("T", 12, 3), ("M", 10), ("M", 11), ("T", 13, 0), ("T", 13, 1), ("T", 13, 2), ("T", 13, 3), ("TF", 3), ("T", 14, 0), ("TM", 3), ("T", 14, 1), ("T", 14, 2), ("T", 14, 3), ("T", 15, 0), ("T", 15, 1), ("T", 15, 2), ("M", 12), ("M", 13), ("T", 15, 3), ("T", 16, 0), ("T", 16, 1), ("T", 16, 2), ("T", 16, 3), ("T", 17, 0), ("TF", 4), ("T", 17, 1), ("T", 17, 2), ("T", 17, 3), ("T", 18, 0), ("T", 18, 1), ("T", 18, 2), ("M", 14), ("M", 15), ("T", 18, 3), ("T", 19, 0), ("T", 19, 1), ("T", 19, 2), ("TM", 4), ("T", 19, 3), ("T", 20, 0), ("T", 20, 1), ("T", 20, 2), ("T", 20, 3), ("M", 16), ("M", 17), ("T", 21, 0), ("T", 21, 1), ("T", 21, 2), ("T", 21, 3), ("TF", 5), ("T", 22, 0), ("TM", 5), ("T", 22, 1), ("T", 22, 2), ("T", 22, 3), ("T", 23, 0), ("T", 23, 1), ("T", 23, 2), ("M", 18), ("M", 19), ("T", 23, 3), ("M", 20), ("M", 21), ("TF", 6), ("M", 22), ("M", 23), ("TM", 6), ("TF", 7), ("TM", 7)]
-        q_s = [("E", 0, 0), ("E", 0, 1), ("E", 0, 2), ("E", 0, 3), ("E", 24, 0), ("E", 24, 1), ("E", 24, 3), ("E", 1, 0), ("E", 1, 1), ("E", 1, 3), ("A", 0), ("E", 2, 0), ("E", 2, 2), ("E", 2, 3), ("A", 1), ("E", 3, 0), ("E", 3, 1), ("E", 3, 3), ("E", 4, 0), ("E", 4, 1), ("E", 4, 2), ("A", 2), ("A", 3), ("E", 5, 0), ("E", 5, 2), ("E", 6, 0), ("E", 6, 1), ("E", 6, 2), ("E", 7, 0), ("E", 7, 1), ("A", 4), ("A", 5), ("E", 7, 3), ("E", 8, 0), ("E", 8, 1), ("E", 8, 2), ("E", 25, 0), ("A", 6), ("A", 7), ("E", 25, 1), ("E", 25, 2), ("A", 8), ("E", 9, 0), ("E", 9, 1), ("E", 9, 2), ("E", 9, 3), ("E", 10, 0), ("E", 10, 1), ("E", 10, 2), ("E", 10, 3), ("E", 11, 0), ("E", 11, 1), ("E", 11, 2), ("A", 9), ("E", 12, 0), ("E", 12, 1), ("E", 12, 3), ("A", 10), ("A", 11), ("E", 13, 0), ("E", 13, 1), ("E", 13, 3), ("E", 14, 0), ("E", 14, 1), ("E", 14, 2), ("E", 14, 3), ("E", 15, 1), ("E", 15, 2), ("A", 12), ("A", 13), ("E", 16, 0), ("E", 16, 1), ("E", 16, 2), ("E", 17, 0), ("E", 17, 1), ("E", 17, 2), ("E", 17, 3), ("E", 18, 1), ("E", 18, 2), ("A", 14), ("A", 15), ("E", 18, 3), ("E", 19, 1), ("E", 19, 2), ("E", 19, 3), ("E", 20, 0), ("E", 20, 1), ("E", 20, 2), ("A", 16), ("A", 17), ("E", 21, 0), ("E", 21, 1), ("E", 21, 3), ("E", 22, 0), ("E", 22, 1), ("E", 22, 2), ("E", 22, 3), ("E", 23, 1), ("E", 23, 2), ("A", 18), ("A", 19), ("A", 20), ("A", 21), ("A", 22), ("A", 23)]
-        q_v = [("B0", 0), ("B2", 0), ("Q", 0), ("E", 24, 2), ("Q", 24), ("E", 1, 2), ("Q", 1), ("E", 2, 1), ("Q", 2), ("E", 3, 2), ("Q", 3), ("E", 4, 3), ("Q", 4), ("G", 0), ("E", 5, 1), ("E", 5, 3), ("Q", 5), ("E", 6, 3), ("Q", 6), ("E", 7, 2), ("G", 1), ("Q", 7), ("E", 8, 3), ("Q", 8), ("F1", 0), ("F2", 0), ("E", 25, 3), ("Q", 25), ("F1", 1), ("G", 2), ("F2", 1), ("F1", 2), ("Q", 9), ("F2", 2), ("Q", 10), ("E", 11, 3), ("Q", 11), ("E", 12, 2), ("Q", 12), ("G", 3), ("E", 13, 2), ("F1", 3), ("Q", 13), ("F2", 3), ("E", 15, 0), ("Q", 14), ("E", 15, 3), ("Q", 15), ("E", 16, 3), ("F1", 4), ("Q", 16), ("E", 18, 0), ("Q", 17), ("G", 4), ("E", 19, 0), ("Q", 18), ("F2", 4), ("Q", 19), ("E", 20, 3), ("Q", 20), ("G", 5), ("E", 21, 2), ("F1", 5), ("Q", 21), ("F2", 5), ("E", 23, 0), ("Q", 22), ("E", 23, 3), ("Q", 23), ("G", 6), ("F1", 6), ("F2", 6), ("F1", 7), ("G", 7), ("F2", 7)]
-        q_g = []
-        queues = [q_sync, q_pe, q_s, q_v, q_g]
+        def quantize_xh(s):
+            cols = slice(s * 256, (s + 1) * 256)
+            nc.vector.quantize_mx(out=x_codes[:, cols].bitcast(FP8X4), scales=x_scales[:, cols], in_=grp["x", s][:])
 
-        needs = {}
+        def new_codes(u):
+            codes[u] = codep.tile([P, 1024], U32, name="cd", align_bytes=64)
+            scales[u] = codep.tile([P, 1024], U8, name="sc", align_bytes=64)
 
-        def need(op, other):
-            needs[op] = needs.get(op, []) + [other]
+        def quantize_columns(u, first, last):
+            cols = slice(first, last)
+            nc.vector.quantize_mx(out=codes[u][:, cols].bitcast(FP8X4), scales=scales[u][:, cols],
+                                  in_=grp[u][:, 4 * first:4 * last])
 
-        def ring(allocs, bufs, users):
-            for i in range(bufs, len(allocs)):
-                for other in users(allocs[i - bufs]):
-                    need(allocs[i], other)
+        def quantize_weight(u):
+            new_codes(u)
+            quantize_columns(u, 0, 1024)
 
-        for job in jobs:
-            for b in range(4):
-                if job >= XJOB:
-                    need(("T", job, b), ("LX", job - XJOB))
-                elif job == 0:
-                    need(("T", job, b), ("LW", 0, b, 4))
-                else:
-                    need(("T", job, b), ("LW", job, 0, 1))
-                need(("E", job, b), ("T", job, b))
-                need(("Q", job), ("E", job, b))
-        for u in range(UNITS):
-            need(("M", u), ("Q", u))
-            need(("M", u), ("Q", XJOB + u // 12))
-            need(("A", u), ("M", u))
-            need(("A", u), ("B2", 0))
-        need(("B1", 0), ("B0", 0))
-        need(("B2", 0), ("B1", 0))
-        for s in range(STREAMS):
-            need(("TF", s), ("A", 3 * s + 1))
-            need(("F1", s), ("TF", s))
-            need(("F1", s), ("LC", 0))
-            need(("G", s), ("A", 3 * s))
-            need(("G", s), ("A", 3 * s + 2))
-            need(("TM", s), ("G", s))
-            need(("F2", s), ("TM", s))
-            need(("F2", s), ("F1", s))
-            need(("ST", s), ("F2", s))
-        ring([op for op in q_sync if op[0] == "LW" and op[2] == 0], RAW_BUFS, lambda o: [("T", o[1], 3)])
-        ring([op for op in q_pe if op[0] == "T"], TP_BUFS, lambda o: [("E", o[1], o[2])])
-        ring([op for op in q_pe if op[0] == "T" and op[2] == 0], GRP_BUFS, lambda o: [("Q", o[1])])
-        ring([op for op in q_v if op[0] == "Q" and op[1] < XJOB], CODE_BUFS, lambda o: [("M", o[1])])
-        ring([op for op in q_pe if op[0] == "M"], ACC_BUFS, lambda o: [("A", o[1])])
-        ring([op for op in q_pe if op[0] in ("B1", "TF", "TM")], TB_BUFS,
-             lambda o: [{"B1": ("B2", 0), "TF": ("F1", o[1]), "TM": ("F2", o[1])}[o[0]]])
-        ring([("A", 3 * s) for s in range(STREAMS)], GATE_BUFS, lambda o: [("G", o[1] // 3)])
-        ring([("A", 3 * s + 1) for s in range(STREAMS)], GATE_BUFS, lambda o: [("TF", o[1] // 3)])
-        ring([("A", 3 * s + 2) for s in range(STREAMS)], GATE_BUFS, lambda o: [("G", o[1] // 3)])
-        ring([("F1", s) for s in range(STREAMS)], GATE_BUFS, lambda o: [("F2", o[1])])
-        ring([("G", s) for s in range(STREAMS)], GATE_BUFS, lambda o: [("TM", o[1])])
+        def multiply_quarter(u, t, dst):
+            s = u // GATES
+            for half in range(2):
+                wc = slice((2 * t + half) * P, (2 * t + half + 1) * P)
+                xc = slice((2 * s + half) * P, (2 * s + half + 1) * P)
+                nc.tensor.matmul_mx(out=dst, lhsT=codes[u][:, wc].bitcast(FP8X4), lhsT_scale=scales[u][:, wc],
+                                    rhs=x_codes[:, xc].bitcast(FP8X4), rhs_scale=x_scales[:, xc],
+                                    start=(half == 0), stop=(half == 1))
+
+        def activate_quarter(u, t, src):
+            s, g = divmod(u, GATES)
+            row = t * UNITS + g * STREAMS + s
+            nc.scalar.activation(out=gate[u][:, t * P:(t + 1) * P], in_=src, func=funcs[g],
+                                 bias=bias_sb[:, row:row + 1])
+
+        def multiply(u):
+            acc[u] = ps_acc.tile([P, 512], F32, name="acc")
+            for t in range(4):
+                multiply_quarter(u, t, acc[u][:, t * P:(t + 1) * P])
+
+        def new_gate(u):
+            gate[u] = gatep.tile([P, 512], F32, name="gate%d" % (u % GATES))
+
+        def activate(u):
+            new_gate(u)
+            for t in range(4):
+                activate_quarter(u, t, acc[u][:, t * P:(t + 1) * P])
+
+        def turn_back(key, src, quarters):
+            if 0 in quarters:
+                back[key] = ps_tb.tile([P, 512], F32, name="tb")
+            for t in quarters:
+                nc.tensor.transpose(out=back[key][:, t * P:(t + 1) * P], in_=src[:, t * P:(t + 1) * P], identity=ident[:])
+
+        def turn_forget(s):
+            turn_back(("f", s), gate[3 * s], range(4))
+
+        def turn_product(s):
+            turn_back(("ig", s), ig[s], range(4))
+
+        def forget_times_c(s):
+            fc[s] = gatep.tile([P, 512], F32, name="fc")
+            nc.vector.tensor_tensor(out=fc[s][:].rearrange("n (p t) -> n p t", t=4),
+                                    in0=back["f", s][:].rearrange("n (t p) -> n p t", t=4),
+                                    in1=c_sb[:, cols_of(s)].rearrange("n (p t) -> n p t", t=4), op=ALU.mult)
+
+        def product_columns(s, cols):
+            nc.vector.tensor_tensor(out=ig[s][:, cols], in0=gate[3 * s + 1][:, cols], in1=gate[3 * s + 2][:, cols],
+                                    op=ALU.mult)
+
+        def new_product(s):
+            ig[s] = gatep.tile([P, 512], F32, name="ig")
+
+        def input_times_candidate(s):
+            new_product(s)
+            product_columns(s, slice(0, 512))
+
+        def add_and_place(s):
+            nc.vector.tensor_tensor(out=o_sb[:, cols_of(s)].rearrange("n (p t) -> n p t", t=4),
+                                    in0=back["ig", s][:].rearrange("n (t p) -> n p t", t=4),
+                                    in1=fc[s][:].rearrange("n (p t) -> n p t", t=4), op=ALU.add)
 
         nc.vector.memset(warm[:], 0.0)
         nc.vector.memset(b_rows[:], 0.0)
@@ -258,16 +198,75 @@ def tile_flatlstm_pa_kernel(tc, modulation, h0, c0, Wi, b_i, Wf, b_f, Wg, b_g, o
         nc.scalar.activation(out=warm[:, 1:2], in_=warm[:, 0:1], func=ACT.Sigmoid)
         make_identity(nc, ident[:])
 
-        done = set()
-        heads = [0 for q in queues]
-        left = sum([len(q) for q in queues])
-        while left > 0:
-            moved = 0
-            for i, q in enumerate(queues):
-                while heads[i] < len(q) and all([o in done for o in needs.get(q[heads[i]], [])]):
-                    emit(q[heads[i]])
-                    done.add(q[heads[i]])
-                    heads[i] += 1
-                    moved += 1
-            assert moved > 0, "the queues wait for each other"
-            left -= moved
+        loads = [(0, load_xh, (0,))]
+        for u in range(UNITS):
+            if u % GATES == 2 and u // GATES + 1 < STREAMS:
+                loads.append((u, load_xh, (u // GATES + 1,)))
+            loads.append((u, load_weight, (u, 2 if u == 0 else 1)))
+            if u % GATES == 0 and u > 0:
+                loads.append((u, load_c, (u // GATES - 1,)))
+        loads.append((UNITS - 1, load_c, (STREAMS - 1,)))
+
+        for r in range(UNITS):
+            for before, load, args in loads:
+                if before == r + RAW_BUFS - 1 or (r == 0 and before < RAW_BUFS):
+                    load(*args)
+            if r == 0:
+                turn_xh(0)
+                quantize_xh(0)
+            else:
+                quantize_weight(r - 1)
+            for b in range(4):
+                turn_weight(r, b)
+            s = (r - 4) // GATES
+            if r >= 4 and r % GATES == 1:
+                turn_forget(s)
+            coming = (r + 2) // GATES
+            turns_xh = r % GATES == 1 and coming < STREAMS
+            if turns_xh:
+                turn_xh(coming)
+            if r >= 6 and r % GATES == 0:
+                turn_product(r // GATES - 2)
+            if r == 0:
+                nc.vector.tensor_copy(out=b_f32[:].rearrange("r (t p) -> r t p", t=4),
+                                      in_=b_rows[:].rearrange("r (p t) -> r t p", t=4))
+            if r == 1:
+                turn_back("b", b_f32, range(4))
+                nc.vector.tensor_copy(out=bias_sb[:].rearrange("p (t r) -> p t r", t=4),
+                                      in_=back["b"][:].rearrange("p (t r) -> p t r", t=4)[:, :, 0:UNITS])
+            if r >= 2:
+                multiply(r - 2)
+                activate(r - 2)
+            if r >= 4:
+                if r % GATES == 1:
+                    forget_times_c(s)
+                elif r % GATES == 2:
+                    input_times_candidate(s)
+                elif r >= 6:
+                    add_and_place(r // GATES - 2)
+            if turns_xh:
+                quantize_xh(coming)
+
+        last = UNITS - 1
+        s = STREAMS - 1
+        multiply(last - 1)
+        activate(last - 1)
+        turn_product(s - 1)
+        new_codes(last)
+        new_gate(last)
+        for t in range(4):
+            quantize_columns(last, t * 256, (t + 1) * 256)
+            quarter = ps_tp.tile([P, 512], F32, name="tp")
+            multiply_quarter(last, t, quarter[:, 0:P])
+            activate_quarter(last, t, quarter[:, 0:P])
+            if t == 1:
+                turn_forget(s)
+        add_and_place(s - 1)
+        forget_times_c(s)
+        new_product(s)
+        for t in range(4):
+            product_columns(s, slice(t * P, (t + 1) * P))
+            turn_back(("ig", s), ig[s], [t])
+        add_and_place(s)
+        for s in range(STREAMS):
+            store(s)

@@ -74,12 +74,15 @@ def tile_flatlstm_pa_kernel(tc, modulation, h0, c0, Wi, b_i, Wf, b_f, Wg, b_g, o
                 nc.sync.dma_start(out=raw[u][:, cols],
                                   in_=weights[g][s].rearrange("(p t) d -> p (t d)", t=4)[:, cols])
 
-        def load_xh(s):
-            nc.sync.dma_start(out=x_sb[:, cols_of(s)], in_=modulation[:, cols_of(s)])
-            nc.sync.dma_start(out=h_sb[:, cols_of(s)], in_=h0[:, cols_of(s)])
+        def half(i):
+            return slice(i * STREAMS // 2 * WIDTH, (i + 1) * STREAMS // 2 * WIDTH)
 
-        def load_c(s):
-            nc.sync.dma_start(out=c_sb[:, cols_of(s)], in_=c0[:, cols_of(s)])
+        def load_xh(i):
+            nc.sync.dma_start(out=x_sb[:, half(i)], in_=modulation[:, half(i)])
+            nc.sync.dma_start(out=h_sb[:, half(i)], in_=h0[:, half(i)])
+
+        def load_c(i):
+            nc.sync.dma_start(out=c_sb[:, half(i)], in_=c0[:, half(i)])
 
         def store(s):
             nc.sync.dma_start(out=out[:, cols_of(s)], in_=o_sb[:, cols_of(s)])
@@ -198,23 +201,23 @@ def tile_flatlstm_pa_kernel(tc, modulation, h0, c0, Wi, b_i, Wf, b_f, Wg, b_g, o
         nc.scalar.activation(out=warm[:, 1:2], in_=warm[:, 0:1], func=ACT.Sigmoid)
         make_identity(nc, ident[:])
 
-        loads = [(0, load_xh, (0,))]
+        loads = []
         for u in range(UNITS):
-            if u % GATES == 2 and u // GATES + 1 < STREAMS:
-                loads.append((u, load_xh, (u // GATES + 1,)))
+            if u == 9:
+                loads.append((u, load_xh, (1,)))
+            if u == 4:
+                loads.append((u, load_c, (0,)))
+            if u == 14:
+                loads.append((u, load_c, (1,)))
             loads.append((u, load_weight, (u, 2 if u == 0 else 1)))
-            if u % GATES == 0 and u > 0:
-                loads.append((u, load_c, (u // GATES - 1,)))
-        loads.append((UNITS - 1, load_c, (STREAMS - 1,)))
+            if u == 0:
+                loads.append((u, load_xh, (0,)))
 
         for r in range(UNITS):
             for before, load, args in loads:
                 if before == r + RAW_BUFS - 1 or (r == 0 and before < RAW_BUFS):
                     load(*args)
-            if r == 0:
-                turn_xh(0)
-                quantize_xh(0)
-            else:
+            if r > 0:
                 quantize_weight(r - 1)
             for b in range(4):
                 turn_weight(r, b)
@@ -228,6 +231,7 @@ def tile_flatlstm_pa_kernel(tc, modulation, h0, c0, Wi, b_i, Wf, b_f, Wg, b_g, o
             if r >= 6 and r % GATES == 0:
                 turn_product(r // GATES - 2)
             if r == 0:
+                turn_xh(0)
                 nc.vector.tensor_copy(out=b_f32[:].rearrange("r (t p) -> r t p", t=4),
                                       in_=b_rows[:].rearrange("r (p t) -> r t p", t=4))
             if r == 1:
@@ -244,6 +248,8 @@ def tile_flatlstm_pa_kernel(tc, modulation, h0, c0, Wi, b_i, Wf, b_f, Wg, b_g, o
                     input_times_candidate(s)
                 elif r >= 6:
                     add_and_place(r // GATES - 2)
+            if r == 0:
+                quantize_xh(0)
             if turns_xh:
                 quantize_xh(coming)
 

@@ -33,8 +33,8 @@ def tile_flatlstm_pa_kernel(tc, modulation, h0, c0, Wi, b_i, Wf, b_f, Wg, b_g, o
         xgrpp = ctx.enter_context(tc.tile_pool(name="xgrpp", bufs=2))
         codep = ctx.enter_context(tc.tile_pool(name="codep", bufs=6))
         gatep = ctx.enter_context(tc.tile_pool(name="gatep", bufs=3))
-        ps_tp = ctx.enter_context(tc.psum_pool(name="ps_tp", bufs=4))
-        ps_acc = ctx.enter_context(tc.psum_pool(name="ps_acc", bufs=2))
+        ps_tp = ctx.enter_context(tc.psum_pool(name="ps_tp", bufs=5))
+        ps_acc = ctx.enter_context(tc.psum_pool(name="ps_acc", bufs=1))
         ps_tb = ctx.enter_context(tc.psum_pool(name="ps_tb", bufs=2))
         ctx.enter_context(tc.manual_schedule())
 
@@ -74,18 +74,18 @@ def tile_flatlstm_pa_kernel(tc, modulation, h0, c0, Wi, b_i, Wf, b_f, Wg, b_g, o
                 nc.sync.dma_start(out=raw[u][:, cols],
                                   in_=weights[g][s].rearrange("(p t) d -> p (t d)", t=4)[:, cols])
 
-        def half(i):
-            return slice(i * STREAMS // 2 * WIDTH, (i + 1) * STREAMS // 2 * WIDTH)
+        def load_xh(first, end):
+            cols = slice(first * WIDTH, end * WIDTH)
+            nc.sync.dma_start(out=x_sb[:, cols], in_=modulation[:, cols])
+            nc.sync.dma_start(out=h_sb[:, cols], in_=h0[:, cols])
 
-        def load_xh(i):
-            nc.sync.dma_start(out=x_sb[:, half(i)], in_=modulation[:, half(i)])
-            nc.sync.dma_start(out=h_sb[:, half(i)], in_=h0[:, half(i)])
+        def load_c(first, end):
+            cols = slice(first * WIDTH, end * WIDTH)
+            nc.sync.dma_start(out=c_sb[:, cols], in_=c0[:, cols])
 
-        def load_c(i):
-            nc.sync.dma_start(out=c_sb[:, half(i)], in_=c0[:, half(i)])
-
-        def store(s):
-            nc.sync.dma_start(out=out[:, cols_of(s)], in_=o_sb[:, cols_of(s)])
+        def store(s, first, end):
+            cols = slice(s * WIDTH + first, s * WIDTH + end)
+            nc.sync.dma_start(out=out[:, cols], in_=o_sb[:, cols])
 
         def turn(srcs):
             tp = ps_tp.tile([P, 512], F32, name="tp")
@@ -106,7 +106,7 @@ def tile_flatlstm_pa_kernel(tc, modulation, h0, c0, Wi, b_i, Wf, b_f, Wg, b_g, o
                 grp[u] = grpp.tile([P, 4096], BF16, name="grp", align_bytes=64)
             words = raw[u][:].bitcast(F32)
             tp = turn([words[:, (4 * b + q) * P:(4 * b + q + 1) * P] for q in range(4)])
-            pack(grp[u], b, tp, b == 2)
+            pack(grp[u], b, tp, b == 3 and u < UNITS - 1)
 
         def turn_xh(s):
             grp["x", s] = xgrpp.tile([P, 1024], BF16, name="xgrp", align_bytes=64)
@@ -148,7 +148,10 @@ def tile_flatlstm_pa_kernel(tc, modulation, h0, c0, Wi, b_i, Wf, b_f, Wg, b_g, o
                                  bias=bias_sb[:, row:row + 1])
 
         def multiply(u):
-            acc[u] = ps_acc.tile([P, 512], F32, name="acc")
+            if u < UNITS - 2:
+                acc[u] = ps_acc.tile([P, 512], F32, name="acc")
+            else:
+                acc[u] = ps_tp.tile([P, 512], F32, name="tp")
             for t in range(4):
                 multiply_quarter(u, t, acc[u][:, t * P:(t + 1) * P])
 
@@ -189,10 +192,10 @@ def tile_flatlstm_pa_kernel(tc, modulation, h0, c0, Wi, b_i, Wf, b_f, Wg, b_g, o
             new_product(s)
             product_columns(s, slice(0, 512))
 
-        def add_and_place(s):
-            nc.vector.tensor_tensor(out=o_sb[:, cols_of(s)].rearrange("n (p t) -> n p t", t=4),
-                                    in0=back["ig", s][:].rearrange("n (t p) -> n p t", t=4),
-                                    in1=fc[s][:].rearrange("n (p t) -> n p t", t=4), op=ALU.add)
+        def add_and_place(s, first, end):
+            nc.vector.tensor_tensor(out=o_sb[:, cols_of(s)].rearrange("n (p t) -> n p t", t=4)[:, first:end, :],
+                                    in0=back["ig", s][:].rearrange("n (t p) -> n p t", t=4)[:, first:end, :],
+                                    in1=fc[s][:].rearrange("n (p t) -> n p t", t=4)[:, first:end, :], op=ALU.add)
 
         nc.vector.memset(warm[:], 0.0)
         nc.vector.memset(b_rows[:], 0.0)
@@ -201,17 +204,12 @@ def tile_flatlstm_pa_kernel(tc, modulation, h0, c0, Wi, b_i, Wf, b_f, Wg, b_g, o
         nc.scalar.activation(out=warm[:, 1:2], in_=warm[:, 0:1], func=ACT.Sigmoid)
         make_identity(nc, ident[:])
 
+        small_loads = {1: [(load_xh, (0, 4))], 4: [(load_c, (0, 4))], 9: [(load_xh, (4, 8))], 14: [(load_c, (4, 7))]}
         loads = []
         for u in range(UNITS):
-            if u == 9:
-                loads.append((u, load_xh, (1,)))
-            if u == 4:
-                loads.append((u, load_c, (0,)))
-            if u == 14:
-                loads.append((u, load_c, (1,)))
+            loads.extend([(u, load, args) for load, args in small_loads.get(u, [])])
             loads.append((u, load_weight, (u, 2 if u == 0 else 1)))
-            if u == 0:
-                loads.append((u, load_xh, (0,)))
+        loads.append((UNITS - 1, load_c, (7, 8)))
 
         for r in range(UNITS):
             for before, load, args in loads:
@@ -247,7 +245,7 @@ def tile_flatlstm_pa_kernel(tc, modulation, h0, c0, Wi, b_i, Wf, b_f, Wg, b_g, o
                 elif r % GATES == 2:
                     input_times_candidate(s)
                 elif r >= 6:
-                    add_and_place(r // GATES - 2)
+                    add_and_place(r // GATES - 2, 0, P)
             if r == 0:
                 quantize_xh(0)
             if turns_xh:
@@ -267,12 +265,14 @@ def tile_flatlstm_pa_kernel(tc, modulation, h0, c0, Wi, b_i, Wf, b_f, Wg, b_g, o
             activate_quarter(last, t, quarter[:, 0:P])
             if t == 1:
                 turn_forget(s)
-        add_and_place(s - 1)
+        add_and_place(s - 1, 0, P)
         forget_times_c(s)
         new_product(s)
         for t in range(4):
             product_columns(s, slice(t * P, (t + 1) * P))
             turn_back(("ig", s), ig[s], [t])
-        add_and_place(s)
-        for s in range(STREAMS):
-            store(s)
+        for i in range(STREAMS - 1):
+            store(i, 0, WIDTH)
+        for i in range(2):
+            add_and_place(s, i * P // 2, (i + 1) * P // 2)
+            store(s, i * WIDTH // 2, (i + 1) * WIDTH // 2)

@@ -33,8 +33,8 @@ def tile_flatlstm_pa_kernel(tc, modulation, h0, c0, Wi, b_i, Wf, b_f, Wg, b_g, o
         xgrpp = ctx.enter_context(tc.tile_pool(name="xgrpp", bufs=2))
         codep = ctx.enter_context(tc.tile_pool(name="codep", bufs=6))
         gatep = ctx.enter_context(tc.tile_pool(name="gatep", bufs=3))
-        ps_tp = ctx.enter_context(tc.psum_pool(name="ps_tp", bufs=5))
-        ps_acc = ctx.enter_context(tc.psum_pool(name="ps_acc", bufs=1))
+        ps_tp = ctx.enter_context(tc.psum_pool(name="ps_tp", bufs=4))
+        ps_acc = ctx.enter_context(tc.psum_pool(name="ps_acc", bufs=2))
         ps_tb = ctx.enter_context(tc.psum_pool(name="ps_tb", bufs=2))
         ctx.enter_context(tc.manual_schedule())
 
@@ -148,10 +148,7 @@ def tile_flatlstm_pa_kernel(tc, modulation, h0, c0, Wi, b_i, Wf, b_f, Wg, b_g, o
                                  bias=bias_sb[:, row:row + 1])
 
         def multiply(u):
-            if u < UNITS - 2:
-                acc[u] = ps_acc.tile([P, 512], F32, name="acc")
-            else:
-                acc[u] = ps_tp.tile([P, 512], F32, name="tp")
+            acc[u] = ps_acc.tile([P, 512], F32, name="acc")
             for t in range(4):
                 multiply_quarter(u, t, acc[u][:, t * P:(t + 1) * P])
 

@@ -201,7 +201,7 @@ def tile_flatlstm_pa_kernel(tc, modulation, h0, c0, Wi, b_i, Wf, b_f, Wg, b_g, o
         nc.scalar.activation(out=warm[:, 1:2], in_=warm[:, 0:1], func=ACT.Sigmoid)
         make_identity(nc, ident[:])
 
-        small_loads = {1: [(load_xh, (0, 4))], 4: [(load_c, (0, 4))], 9: [(load_xh, (4, 8))], 14: [(load_c, (4, 7))]}
+        small_loads = {2: [(load_xh, (0, 4))], 5: [(load_c, (0, 4))], 13: [(load_xh, (4, 8))], 16: [(load_c, (4, 7))]}
         loads = []
         for u in range(UNITS):
             loads.extend([(u, load, args) for load, args in small_loads.get(u, [])])
@@ -219,17 +219,14 @@ def tile_flatlstm_pa_kernel(tc, modulation, h0, c0, Wi, b_i, Wf, b_f, Wg, b_g, o
             s = (r - 4) // GATES
             if r >= 4 and r % GATES == 1:
                 turn_forget(s)
-            coming = (r + 2) // GATES
-            turns_xh = r % GATES == 1 and coming < STREAMS
-            if turns_xh:
-                turn_xh(coming)
+            if r % GATES == 1:
+                turn_xh(r // GATES)
             if r >= 6 and r % GATES == 0:
                 turn_product(r // GATES - 2)
-            if r == 0:
-                turn_xh(0)
+            if r == 1:
                 nc.vector.tensor_copy(out=b_f32[:].rearrange("r (t p) -> r t p", t=4),
                                       in_=b_rows[:].rearrange("r (p t) -> r t p", t=4))
-            if r == 1:
+            if r == 2:
                 turn_back("b", b_f32, range(4))
                 nc.vector.tensor_copy(out=bias_sb[:].rearrange("p (t r) -> p t r", t=4),
                                       in_=back["b"][:].rearrange("p (t r) -> p t r", t=4)[:, :, 0:UNITS])
@@ -243,10 +240,8 @@ def tile_flatlstm_pa_kernel(tc, modulation, h0, c0, Wi, b_i, Wf, b_f, Wg, b_g, o
                     input_times_candidate(s)
                 elif r >= 6:
                     add_and_place(r // GATES - 2, 0, P)
-            if r == 0:
-                quantize_xh(0)
-            if turns_xh:
-                quantize_xh(coming)
+            if r % GATES == 1:
+                quantize_xh(r // GATES)
 
         last = UNITS - 1
         s = STREAMS - 1

@@ -87,6 +87,11 @@ def tile_flatlstm_pa_kernel(tc, modulation, h0, c0, Wi, b_i, Wf, b_f, Wg, b_g, o
             cols = slice(s * WIDTH + first, s * WIDTH + end)
             nc.sync.dma_start(out=out[:, cols], in_=o_sb[:, cols])
 
+        def keep_clock(count, lhsT, rhs):
+            idle = ps_acc.tile([P, 512], F32, name="acc")
+            for i in range(count):
+                nc.tensor.matmul(out=idle[:, 0:rhs.shape[1]], lhsT=lhsT, rhs=rhs, start=True, stop=True)
+
         def turn(srcs):
             tp = ps_tp.tile([P, 512], F32, name="tp")
             for q in range(4):
@@ -200,8 +205,10 @@ def tile_flatlstm_pa_kernel(tc, modulation, h0, c0, Wi, b_i, Wf, b_f, Wg, b_g, o
             nc.scalar.dma_start(out=b_rows[8 * g:8 * g + 8, :], in_=biases[g])
         nc.scalar.activation(out=warm[:, 1:2], in_=warm[:, 0:1], func=ACT.Sigmoid)
         make_identity(nc, ident[:])
+        keep_clock(3, ident[:], ident[:])
 
-        small_loads = {2: [(load_xh, (0, 4))], 5: [(load_c, (0, 4))], 13: [(load_xh, (4, 8))], 16: [(load_c, (4, 7))]}
+        small_loads = {2: [(load_xh, (0, 2))], 5: [(load_c, (0, 2))], 7: [(load_xh, (2, 4))], 11: [(load_c, (2, 4))],
+                       13: [(load_xh, (4, 6))], 17: [(load_c, (4, 7))], 19: [(load_xh, (6, 8))]}
         loads = []
         for u in range(UNITS):
             loads.extend([(u, load, args) for load, args in small_loads.get(u, [])])
@@ -226,10 +233,10 @@ def tile_flatlstm_pa_kernel(tc, modulation, h0, c0, Wi, b_i, Wf, b_f, Wg, b_g, o
             if r == 1:
                 nc.vector.tensor_copy(out=b_f32[:].rearrange("r (t p) -> r t p", t=4),
                                       in_=b_rows[:].rearrange("r (p t) -> r t p", t=4))
-            if r == 2:
+                keep_clock(3, raw[r][:, 0:P], raw[r][:, 0:512])
                 turn_back("b", b_f32, range(4))
-                nc.vector.tensor_copy(out=bias_sb[:].rearrange("p (t r) -> p t r", t=4),
-                                      in_=back["b"][:].rearrange("p (t r) -> p t r", t=4)[:, :, 0:UNITS])
+            if r == 0:
+                keep_clock(3, raw[r][:, 0:P], raw[r][:, 0:512])
             if r >= 2:
                 multiply(r - 2)
                 activate(r - 2)
@@ -242,6 +249,9 @@ def tile_flatlstm_pa_kernel(tc, modulation, h0, c0, Wi, b_i, Wf, b_f, Wg, b_g, o
                     add_and_place(r // GATES - 2, 0, P)
             if r % GATES == 1:
                 quantize_xh(r // GATES)
+            if r == 1:
+                nc.vector.tensor_copy(out=bias_sb[:].rearrange("p (t r) -> p t r", t=4),
+                                      in_=back["b"][:].rearrange("p (t r) -> p t r", t=4)[:, :, 0:UNITS])
 
         last = UNITS - 1
         s = STREAMS - 1

@@ -152,8 +152,10 @@ def tile_flatlstm_pa_kernel(tc, modulation, h0, c0, Wi, b_i, Wf, b_f, Wg, b_g, o
             nc.scalar.activation(out=gate[u][:, t * P:(t + 1) * P], in_=src, func=funcs[g],
                                  bias=bias_sb[:, row:row + 1])
 
-        def multiply(u):
+        def new_acc(u):
             acc[u] = ps_acc.tile([P, 512], F32, name="acc")
+
+        def multiply(u):
             for t in range(4):
                 multiply_quarter(u, t, acc[u][:, t * P:(t + 1) * P])
 
@@ -223,6 +225,9 @@ def tile_flatlstm_pa_kernel(tc, modulation, h0, c0, Wi, b_i, Wf, b_f, Wg, b_g, o
                 quantize_weight(r - 1)
             for b in range(4):
                 turn_weight(r, b)
+                if r >= 2 and b == 1:
+                    new_acc(r - 2)
+                    nc.tensor.matmul(out=acc[r - 2][:, 0:P], lhsT=ident[:], rhs=ident[:], start=True, stop=True)
             s = (r - 4) // GATES
             if r >= 4 and r % GATES == 1:
                 turn_forget(s)
@@ -255,6 +260,7 @@ def tile_flatlstm_pa_kernel(tc, modulation, h0, c0, Wi, b_i, Wf, b_f, Wg, b_g, o
 
         last = UNITS - 1
         s = STREAMS - 1
+        new_acc(last - 1)
         multiply(last - 1)
         activate(last - 1)
         turn_product(s - 1)

@@ -227,7 +227,7 @@ def tile_flatlstm_pa_kernel(tc, modulation, h0, c0, Wi, b_i, Wf, b_f, Wg, b_g, o
                 turn_weight(r, b)
                 if r >= 2 and b == 1:
                     new_acc(r - 2)
-                    nc.tensor.matmul(out=acc[r - 2][:, 0:P], lhsT=ident[:], rhs=ident[:], start=True, stop=True)
+                    nc.tensor.matmul(out=acc[r - 2][:, 0:64], lhsT=ident[:], rhs=ident[:, 0:64], start=True, stop=True)
             s = (r - 4) // GATES
             if r >= 4 and r % GATES == 1:
                 turn_forget(s)

@@ -209,8 +209,9 @@ def tile_flatlstm_pa_kernel(tc, modulation, h0, c0, Wi, b_i, Wf, b_f, Wg, b_g, o
         make_identity(nc, ident[:])
         keep_clock(3, ident[:], ident[:])
 
-        small_loads = {2: [(load_xh, (0, 2))], 5: [(load_c, (0, 2))], 7: [(load_xh, (2, 4))], 11: [(load_c, (2, 4))],
-                       13: [(load_xh, (4, 6))], 17: [(load_c, (4, 7))], 19: [(load_xh, (6, 8))]}
+        small_loads = {1: [(load_xh, (0, 2))], 5: [(load_c, (0, 2))], 7: [(load_xh, (2, 4))], 11: [(load_c, (2, 4))],
+                       13: [(load_xh, (4, 6))], 17: [(load_c, (4, 6))], 19: [(load_xh, (6, 7))], 22: [(load_xh, (7, 8))],
+                       23: [(load_c, (6, 7))]}
         loads = []
         for u in range(UNITS):
             loads.extend([(u, load, args) for load, args in small_loads.get(u, [])])

@@ -209,9 +209,7 @@ def tile_flatlstm_pa_kernel(tc, modulation, h0, c0, Wi, b_i, Wf, b_f, Wg, b_g, o
         make_identity(nc, ident[:])
         keep_clock(3, ident[:], ident[:])
 
-        small_loads = {1: [(load_xh, (0, 2))], 5: [(load_c, (0, 2))], 7: [(load_xh, (2, 4))], 11: [(load_c, (2, 4))],
-                       13: [(load_xh, (4, 6))], 17: [(load_c, (4, 6))], 19: [(load_xh, (6, 7))], 22: [(load_xh, (7, 8))],
-                       23: [(load_c, (6, 7))]}
+        small_loads = {2: [(load_xh, (0, 2))], 5: [(load_c, (0, 2))], 8: [(load_xh, (2, 4))], 11: [(load_c, (2, 4))], 14: [(load_xh, (4, 6))], 17: [(load_c, (4, 6))], 20: [(load_xh, (6, 7))], 23: [(load_xh, (7, 8)), (load_c, (6, 7))]}
         loads = []
         for u in range(UNITS):
             loads.extend([(u, load, args) for load, args in small_loads.get(u, [])])

@@ -152,10 +152,8 @@ def tile_flatlstm_pa_kernel(tc, modulation, h0, c0, Wi, b_i, Wf, b_f, Wg, b_g, o
             nc.scalar.activation(out=gate[u][:, t * P:(t + 1) * P], in_=src, func=funcs[g],
                                  bias=bias_sb[:, row:row + 1])
 
-        def new_acc(u):
-            acc[u] = ps_acc.tile([P, 512], F32, name="acc")
-
         def multiply(u):
+            acc[u] = ps_acc.tile([P, 512], F32, name="acc")
             for t in range(4):
                 multiply_quarter(u, t, acc[u][:, t * P:(t + 1) * P])
 
@@ -209,7 +207,8 @@ def tile_flatlstm_pa_kernel(tc, modulation, h0, c0, Wi, b_i, Wf, b_f, Wg, b_g, o
         make_identity(nc, ident[:])
         keep_clock(3, ident[:], ident[:])
 
-        small_loads = {2: [(load_xh, (0, 2))], 5: [(load_c, (0, 2))], 8: [(load_xh, (2, 4))], 11: [(load_c, (2, 4))], 14: [(load_xh, (4, 6))], 17: [(load_c, (4, 6))], 20: [(load_xh, (6, 7))], 23: [(load_xh, (7, 8)), (load_c, (6, 7))]}
+        small_loads = {2: [(load_xh, (0, 3))], 5: [(load_c, (0, 3))], 11: [(load_xh, (3, 6))], 14: [(load_c, (3, 6))],
+                       20: [(load_xh, (6, 8))], 23: [(load_c, (6, 7))]}
         loads = []
         for u in range(UNITS):
             loads.extend([(u, load, args) for load, args in small_loads.get(u, [])])
@@ -224,9 +223,6 @@ def tile_flatlstm_pa_kernel(tc, modulation, h0, c0, Wi, b_i, Wf, b_f, Wg, b_g, o
                 quantize_weight(r - 1)
             for b in range(4):
                 turn_weight(r, b)
-                if r >= 2 and b == 1:
-                    new_acc(r - 2)
-                    nc.tensor.matmul(out=acc[r - 2][:, 0:64], lhsT=ident[:], rhs=ident[:, 0:64], start=True, stop=True)
             s = (r - 4) // GATES
             if r >= 4 and r % GATES == 1:
                 turn_forget(s)
@@ -259,7 +255,6 @@ def tile_flatlstm_pa_kernel(tc, modulation, h0, c0, Wi, b_i, Wf, b_f, Wg, b_g, o
 
         last = UNITS - 1
         s = STREAMS - 1
-        new_acc(last - 1)
         multiply(last - 1)
         activate(last - 1)
         turn_product(s - 1)

@@ -30,7 +30,7 @@ def tile_flatlstm_pa_kernel(tc, modulation, h0, c0, Wi, b_i, Wf, b_f, Wg, b_g, o
         const = ctx.enter_context(tc.tile_pool(name="const", bufs=1))
         rawp = ctx.enter_context(tc.tile_pool(name="rawp", bufs=RAW_BUFS))
         grpp = ctx.enter_context(tc.tile_pool(name="grpp", bufs=4))
-        xgrpp = ctx.enter_context(tc.tile_pool(name="xgrpp", bufs=2))
+        xgrpp = ctx.enter_context(tc.tile_pool(name="xgrpp", bufs=3))
         codep = ctx.enter_context(tc.tile_pool(name="codep", bufs=6))
         gatep = ctx.enter_context(tc.tile_pool(name="gatep", bufs=3))
         ps_tp = ctx.enter_context(tc.psum_pool(name="ps_tp", bufs=4))
@@ -215,6 +215,10 @@ def tile_flatlstm_pa_kernel(tc, modulation, h0, c0, Wi, b_i, Wf, b_f, Wg, b_g, o
             loads.append((u, load_weight, (u, 2 if u == 0 else 1)))
         loads.append((UNITS - 1, load_c, (7, 8)))
 
+        def arrived(r):
+            s, g = divmod(r, GATES)
+            return range(s, min(s + 3, STREAMS)) if g == 1 and s % 3 == 0 else ()
+
         for r in range(UNITS):
             for before, load, args in loads:
                 if before == r + RAW_BUFS - 1 or (r == 0 and before < RAW_BUFS):
@@ -226,8 +230,8 @@ def tile_flatlstm_pa_kernel(tc, modulation, h0, c0, Wi, b_i, Wf, b_f, Wg, b_g, o
             s = (r - 4) // GATES
             if r >= 4 and r % GATES == 1:
                 turn_forget(s)
-            if r % GATES == 1:
-                turn_xh(r // GATES)
+            for x in arrived(r):
+                turn_xh(x)
             if r >= 6 and r % GATES == 0:
                 turn_product(r // GATES - 2)
             if r == 1:
@@ -247,8 +251,8 @@ def tile_flatlstm_pa_kernel(tc, modulation, h0, c0, Wi, b_i, Wf, b_f, Wg, b_g, o
                     input_times_candidate(s)
                 elif r >= 6:
                     add_and_place(r // GATES - 2, 0, P)
-            if r % GATES == 1:
-                quantize_xh(r // GATES)
+            for x in arrived(r):
+                quantize_xh(x)
             if r == 1:
                 nc.vector.tensor_copy(out=bias_sb[:].rearrange("p (t r) -> p t r", t=4),
                                       in_=back["b"][:].rearrange("p (t r) -> p t r", t=4)[:, :, 0:UNITS])

from contextlib import ExitStack

import concourse.mybir as mybir
from concourse.masks import make_identity

F32 = mybir.dt.float32
BF16 = mybir.dt.bfloat16
U32 = mybir.dt.uint32
U8 = mybir.dt.uint8
FP8X4 = mybir.dt.float8_e4m3fn_x4
ACT = mybir.ActivationFunctionType
ALU = mybir.AluOpType

P = 128
STREAMS = 8
WIDTH = 512
GATES = 3
UNITS = STREAMS * GATES
FLOPS = 2 * P * UNITS * WIDTH * 2 * WIDTH

RAW_BUFS = 10


def tile_flatlstm_pa_kernel(tc, modulation, h0, c0, Wi, b_i, Wf, b_f, Wg, b_g, out):
    nc = tc.nc
    weights = (Wf, Wi, Wg)
    biases = (b_f, b_i, b_g)
    funcs = (ACT.Sigmoid, ACT.Sigmoid, ACT.Tanh)
    with ExitStack() as ctx:
        const = ctx.enter_context(tc.tile_pool(name="const", bufs=1))
        rawp = ctx.enter_context(tc.tile_pool(name="rawp", bufs=RAW_BUFS))
        grpp = ctx.enter_context(tc.tile_pool(name="grpp", bufs=4))
        xgrpp = ctx.enter_context(tc.tile_pool(name="xgrpp", bufs=3))
        codep = ctx.enter_context(tc.tile_pool(name="codep", bufs=6))
        gatep = ctx.enter_context(tc.tile_pool(name="gatep", bufs=3))
        ps_tp = ctx.enter_context(tc.psum_pool(name="ps_tp", bufs=4))
        ps_acc = ctx.enter_context(tc.psum_pool(name="ps_acc", bufs=2))
        ps_tb = ctx.enter_context(tc.psum_pool(name="ps_tb", bufs=2))
        ctx.enter_context(tc.manual_schedule())

        ident = const.tile([P, P], F32, name="ident")
        x_sb = const.tile([P, STREAMS * WIDTH], BF16, name="x_sb")
        h_sb = const.tile([P, STREAMS * WIDTH], BF16, name="h_sb")
        c_sb = const.tile([P, STREAMS * WIDTH], BF16, name="c_sb")
        o_sb = const.tile([P, STREAMS * WIDTH], F32, name="o_sb")
        x_codes = const.tile([P, STREAMS * 256], U32, name="x_codes", align_bytes=64)
        x_scales = const.tile([P, STREAMS * 256], U8, name="x_scales", align_bytes=64)
        b_rows = const.tile([P, WIDTH], BF16, name="b_rows")
        b_f32 = const.tile([P, WIDTH], F32, name="b_f32")
        bias_sb = const.tile([P, 4 * UNITS], F32, name="bias_sb")
        warm = const.tile([P, 2], F32, name="warm")
        x_words = x_sb[:].bitcast(F32)
        h_words = h_sb[:].bitcast(F32)

        raw = {}
        grp = {}
        codes = {}
        scales = {}
        acc = {}
        gate = {}
        back = {}
        fc = {}
        ig = {}

        def cols_of(s):
            return slice(s * WIDTH, (s + 1) * WIDTH)

        def load_weight(u, pieces):
            s, g = divmod(u, GATES)
            raw[u] = rawp.tile([P, 4096], BF16, name="raw")
            w = 4096 // pieces
            for i in range(pieces):
                cols = slice(i * w, (i + 1) * w)
                nc.sync.dma_start(out=raw[u][:, cols],
                                  in_=weights[g][s].rearrange("(p t) d -> p (t d)", t=4)[:, cols])

        def load_xh(first, end):
            cols = slice(first * WIDTH, end * WIDTH)
            nc.sync.dma_start(out=x_sb[:, cols], in_=modulation[:, cols])
            nc.sync.dma_start(out=h_sb[:, cols], in_=h0[:, cols])

        def load_c(first, end):
            cols = slice(first * WIDTH, end * WIDTH)
            nc.sync.dma_start(out=c_sb[:, cols], in_=c0[:, cols])

        def store(s, first, end):
            cols = slice(s * WIDTH + first, s * WIDTH + end)
            nc.sync.dma_start(out=out[:, cols], in_=o_sb[:, cols])

        def keep_clock(count, lhsT, rhs):
            idle = ps_acc.tile([P, 512], F32, name="acc")
            for i in range(count):
                nc.tensor.matmul(out=idle[:, 0:rhs.shape[1]], lhsT=lhsT, rhs=rhs, start=True, stop=True)

        def turn(srcs):
            tp = ps_tp.tile([P, 512], F32, name="tp")
            for q in range(4):
                nc.tensor.transpose(out=tp[:, q * P:(q + 1) * P], in_=srcs[q], identity=ident[:])
            return tp

        def pack(dst_tile, b, tp, on_vector):
            dst = dst_tile[:].bitcast(F32)[:, b * 512:(b + 1) * 512].rearrange("p (g c u) -> p g c u", g=2, u=2)
            src = tp[:].rearrange("p (g u c) -> p g c u", g=2, u=2)
            if on_vector:
                nc.vector.tensor_copy(out=dst, in_=src)
            else:
                nc.scalar.copy(out=dst, in_=src)

        def turn_weight(u, b):
            if b == 0:
                grp[u] = grpp.tile([P, 4096], BF16, name="grp", align_bytes=64)
            words = raw[u][:].bitcast(F32)
            tp = turn([words[:, (4 * b + q) * P:(4 * b + q + 1) * P] for q in range(4)])
            pack(grp[u], b, tp, b == 3 and u < UNITS - 1)

        def turn_xh(s):
            grp["x", s] = xgrpp.tile([P, 1024], BF16, name="xgrp", align_bytes=64)
            lo = slice(s * 256, s * 256 + P)
            hi = slice(s * 256 + P, (s + 1) * 256)
            tp = turn([x_words[:, lo], x_words[:, hi], h_words[:, lo], h_words[:, hi]])
            pack(grp["x", s], 0, tp, False)

        def quantize_xh(s):
            cols = slice(s * 256, (s + 1) * 256)
            nc.vector.quantize_mx(out=x_codes[:, cols].bitcast(FP8X4), scales=x_scales[:, cols], in_=grp["x", s][:])

        def new_codes(u):
            codes[u] = codep.tile([P, 1024], U32, name="cd", align_bytes=64)
            scales[u] = codep.tile([P, 1024], U8, name="sc", align_bytes=64)

        def quantize_columns(u, first, last):
            cols = slice(first, last)
            nc.vector.quantize_mx(out=codes[u][:, cols].bitcast(FP8X4), scales=scales[u][:, cols],
                                  in_=grp[u][:, 4 * first:4 * last])

        def quantize_weight(u):
            new_codes(u)
            quantize_columns(u, 0, 1024)

        def multiply_quarter(u, t, dst):
            s = u // GATES
            for half in range(2):
                wc = slice((2 * t + half) * P, (2 * t + half + 1) * P)
                xc = slice((2 * s + half) * P, (2 * s + half + 1) * P)
                nc.tensor.matmul_mx(out=dst, lhsT=codes[u][:, wc].bitcast(FP8X4), lhsT_scale=scales[u][:, wc],
                                    rhs=x_codes[:, xc].bitcast(FP8X4), rhs_scale=x_scales[:, xc],
                                    start=(half == 0), stop=(half == 1))

        def activate_quarter(u, t, src):
            s, g = divmod(u, GATES)
            row = t * UNITS + g * STREAMS + s
            nc.scalar.activation(out=gate[u][:, t * P:(t + 1) * P], in_=src, func=funcs[g],
                                 bias=bias_sb[:, row:row + 1])

        def multiply(u):
            acc[u] = ps_acc.tile([P, 512], F32, name="acc")
            for t in range(4):
                multiply_quarter(u, t, acc[u][:, t * P:(t + 1) * P])

        def new_gate(u):
            gate[u] = gatep.tile([P, 512], F32, name="gate%d" % (u % GATES))

        def activate(u):
            new_gate(u)
            for t in range(4):
                activate_quarter(u, t, acc[u][:, t * P:(t + 1) * P])

        def turn_back(key, src, quarters):
            if 0 in quarters:
                back[key] = ps_tb.tile([P, 512], F32, name="tb")
            for t in quarters:
                nc.tensor.transpose(out=back[key][:, t * P:(t + 1) * P], in_=src[:, t * P:(t + 1) * P], identity=ident[:])

        def turn_forget(s):
            turn_back(("f", s), gate[3 * s], range(4))

        def turn_product(s):
            turn_back(("ig", s), ig[s], range(4))

        def forget_times_c(s):
            fc[s] = gatep.tile([P, 512], F32, name="fc")
            nc.vector.tensor_tensor(out=fc[s][:].rearrange("n (p t) -> n p t", t=4),
                                    in0=back["f", s][:].rearrange("n (t p) -> n p t", t=4),
                                    in1=c_sb[:, cols_of(s)].rearrange("n (p t) -> n p t", t=4), op=ALU.mult)

        def product_columns(s, cols):
            nc.vector.tensor_tensor(out=ig[s][:, cols], in0=gate[3 * s + 1][:, cols], in1=gate[3 * s + 2][:, cols],
                                    op=ALU.mult)

        def new_product(s):
            ig[s] = gatep.tile([P, 512], F32, name="ig")

        def input_times_candidate(s):
            new_product(s)
            product_columns(s, slice(0, 512))

        def add_and_place(s, first, end):
            nc.vector.tensor_tensor(out=o_sb[:, cols_of(s)].rearrange("n (p t) -> n p t", t=4)[:, first:end, :],
                                    in0=back["ig", s][:].rearrange("n (t p) -> n p t", t=4)[:, first:end, :],
                                    in1=fc[s][:].rearrange("n (p t) -> n p t", t=4)[:, first:end, :], op=ALU.add)

        nc.vector.memset(warm[:], 0.0)
        nc.vector.memset(b_rows[:], 0.0)
        for g in range(GATES):
            nc.scalar.dma_start(out=b_rows[8 * g:8 * g + 8, :], in_=biases[g])
        nc.scalar.activation(out=warm[:, 1:2], in_=warm[:, 0:1], func=ACT.Sigmoid)
        make_identity(nc, ident[:])
        keep_clock(3, ident[:], ident[:])

        small_loads = {2: [(load_xh, (0, 3))], 5: [(load_c, (0, 3))], 11: [(load_xh, (3, 6))], 14: [(load_c, (3, 6))],
                       20: [(load_xh, (6, 8))], 23: [(load_c, (6, 7))]}
        loads = []
        for u in range(UNITS):
            loads.extend([(u, load, args) for load, args in small_loads.get(u, [])])
            loads.append((u, load_weight, (u, 2 if u == 0 else 1)))
        loads.append((UNITS - 1, load_c, (7, 8)))

        def arrived(r):
            s, g = divmod(r, GATES)
            return range(s, min(s + 3, STREAMS)) if g == 1 and s % 3 == 0 else ()

        for r in range(UNITS):
            for before, load, args in loads:
                if before == r + RAW_BUFS - 1 or (r == 0 and before < RAW_BUFS):
                    load(*args)
            if r > 0:
                quantize_weight(r - 1)
            for b in range(4):
                turn_weight(r, b)
            s = (r - 4) // GATES
            if r >= 4 and r % GATES == 1:
                turn_forget(s)
            for x in arrived(r):
                turn_xh(x)
            if r >= 6 and r % GATES == 0:
                turn_product(r // GATES - 2)
            if r == 1:
                nc.vector.tensor_copy(out=b_f32[:].rearrange("r (t p) -> r t p", t=4),
                                      in_=b_rows[:].rearrange("r (p t) -> r t p", t=4))
                keep_clock(3, raw[r][:, 0:P], raw[r][:, 0:512])
                turn_back("b", b_f32, range(4))
            if r == 0:
                keep_clock(3, raw[r][:, 0:P], raw[r][:, 0:512])
            if r >= 2:
                multiply(r - 2)
                activate(r - 2)
            if r >= 4:
                if r % GATES == 1:
                    forget_times_c(s)
                elif r % GATES == 2:
                    input_times_candidate(s)
                elif r >= 6:
                    add_and_place(r // GATES - 2, 0, P)
            for x in arrived(r):
                quantize_xh(x)
            if r == 1:
                nc.vector.tensor_copy(out=bias_sb[:].rearrange("p (t r) -> p t r", t=4),
                                      in_=back["b"][:].rearrange("p (t r) -> p t r", t=4)[:, :, 0:UNITS])

        last = UNITS - 1
        s = STREAMS - 1
        multiply(last - 1)
        activate(last - 1)
        turn_product(s - 1)
        new_codes(last)
        new_gate(last)
        for t in range(4):
            quantize_columns(last, t * 256, (t + 1) * 256)
            quarter = ps_tp.tile([P, 512], F32, name="tp")
            multiply_quarter(last, t, quarter[:, 0:P])
            activate_quarter(last, t, quarter[:, 0:P])
            if t == 1:
                turn_forget(s)
        add_and_place(s - 1, 0, P)
        forget_times_c(s)
        new_product(s)
        for t in range(4):
            product_columns(s, slice(t * P, (t + 1) * P))
            turn_back(("ig", s), ig[s], [t])
        for i in range(STREAMS - 1):
            store(i, 0, WIDTH)
        for i in range(2):
            add_and_place(s, i * P // 2, (i + 1) * P // 2)
            store(s, i * WIDTH // 2, (i + 1) * WIDTH // 2)
